import numpy as np
import ml_dtypes


def mxq(x, axis, fmt="e4m3"):
    dtype, down = {"e4m3": (ml_dtypes.float8_e4m3fn, 7), "e5m2": (ml_dtypes.float8_e5m2, 14)}[fmt]
    v = np.moveaxis(np.asarray(x, np.float32).astype(ml_dtypes.bfloat16).astype(np.float64), axis, -1)
    blocks = v.reshape(v.shape[:-1] + (-1, 32))
    amax = np.abs(blocks).max(-1, keepdims=True)
    byte = np.maximum(np.where(amax > 0, np.frexp(amax)[1] - 1 + 127, 0) - down, 1)
    scale = np.exp2(byte - 127.0)
    codes = (blocks / scale).astype(np.float32).astype(dtype).astype(np.float64)
    return np.moveaxis((codes * scale).reshape(v.shape), -1, axis)


WIDE = False


def mx_kscale(k):
    if not WIDE:
        return np.ones(k)
    levels = np.array([10, -10, 5, -5, 0])
    a = np.random.permutation(np.resize(levels, k // 512 * 4)).reshape(k // 512, 4)
    idx = np.arange(k)
    return np.exp2(a[idx // 512, idx % 128 // 32])


BF16 = ml_dtypes.bfloat16


def bf(x):
    return np.asarray(x, np.float32).astype(BF16)


def f64(x):
    return np.asarray(x).astype(np.float64)


T, B, D, U, V, E = 4, 256, 512, 512, 512, 8
G = 2 * E


def softmax(v):
    e = np.exp(v - v.max(-1, keepdims=True))
    return e / e.sum(-1, keepdims=True)


def setup_inputs():
    rn = np.random.standard_normal
    s = mx_kscale(U)
    return {
        "task_h": bf(np.abs(rn((T, B, U))) * 0.55 * s),
        "share_h": bf(np.abs(rn((B, U))) * 0.5 * s),
        "ews1": bf(rn((U, V, E)) * 2.0 / np.sqrt(U) / s[:, None, None]),
        "ebs1": bf(rn((V, E)) * 0.5),
        "ew1": bf(rn((T, U, V, E)) * 2.0 / np.sqrt(U) / s[None, :, None, None]),
        "eb1": bf(rn((T, V, E)) * 0.5),
        "gate_pre1": bf(rn((T, B, G))),
        "gb1": bf(rn((T, G)) * 0.5),
    }


def reference(task_h, share_h, ews1, ebs1, ew1, eb1, gate_pre1, gb1):
    es = np.maximum((mxq(f64(share_h), 1, "e4m3") @ mxq(f64(ews1).reshape(U, V * E), 0, "e4m3")).reshape(B, V, E) + f64(ebs1), 0.0)
    et = np.maximum((mxq(f64(task_h), 2, "e4m3") @ mxq(f64(ew1).reshape(T, U, V * E), 1, "e4m3")).reshape(T, B, V, E) + f64(eb1)[:, None], 0.0)
    g = softmax(f64(gate_pre1) + f64(gb1)[:, None])
    comb = np.concatenate([et, np.broadcast_to(es, et.shape)], axis=-1)
    return (comb * g[:, :, None, :]).sum(-1)

@@ -1,0 +1,262 @@
+from contextlib import ExitStack
+
+import concourse.mybir as mybir
+from concourse.masks import make_identity
+
+F32 = mybir.dt.float32
+BF16 = mybir.dt.bfloat16
+U32 = mybir.dt.uint32
+U8 = mybir.dt.uint8
+FP8X4 = mybir.dt.float8_e4m3fn_x4
+ALU = mybir.AluOpType
+ACT = mybir.ActivationFunctionType
+AXIS = mybir.AxisListType
+
+T, B, U, V, E = 4, 256, 512, 512, 8
+G = 2 * E
+FLOPS = 2 * (T + 1) * B * U * V * E
+
+P = 128
+PACK = 4
+assert U == P * PACK
+
+SHARED = T
+B_TILES = B // P
+V_TILES = V // P
+HALF = E // 2
+ROUNDS = T * 2
+assert ROUNDS == E
+VECTOR_EVERY = 3
+
+
+def tile_plelayer_pb_kernel(tc, task_h, share_h, ews1, ebs1, ew1, eb1, gate_pre1, gb1, out):
+    nc = tc.nc
+    with ExitStack() as stack:
+        keep = stack.enter_context(tc.tile_pool(name="keep", bufs=1))
+        stage = stack.enter_context(tc.tile_pool(name="stage", bufs=2))
+        raw_pool = stack.enter_context(tc.tile_pool(name="raw", bufs=2))
+        grouped_pool = stack.enter_context(tc.tile_pool(name="grouped", bufs=2))
+        own_pool = stack.enter_context(tc.tile_pool(name="own", bufs=3))
+        relu_pool = stack.enter_context(tc.tile_pool(name="relu", bufs=3))
+        psum = stack.enter_context(tc.psum_pool(name="psum", bufs=4))
+
+        identity = keep.tile([P, P], F32)
+        make_identity(nc, identity[:])
+
+        def load_matrix(weights):
+            raw = raw_pool.tile([P, PACK, V * E], BF16, tag="raw")
+            rows = weights.rearrange("(p t) v e -> p t (v e)", t=PACK)
+            for vt in range(V_TILES):
+                cols = slice(vt * P * E, (vt + 1) * P * E)
+                nc.sync.dma_start(out=raw[:, :, cols], in_=rows[:, :, cols])
+            return raw
+
+        acts = keep.tile([P, (T + 1) * B_TILES * U], BF16)
+        acts_by_stream = acts[:].rearrange("p (m h u) -> p m h u", m=T + 1, h=B_TILES)
+        nc.sync.dma_start(out=acts_by_stream[:, SHARED], in_=share_h.rearrange("(h p) u -> p h u", p=P))
+        shared_raw = load_matrix(ews1)
+        nc.sync.dma_start(
+            out=acts_by_stream[:, 0:T].rearrange("p m h u -> p (m h) u"),
+            in_=task_h.rearrange("t (h p) u -> p (t h) u", p=P),
+        )
+        task_raw = {0: load_matrix(ew1[0])}
+
+        gate_in = keep.tile([P, T, B_TILES, G], BF16)
+        nc.scalar.dma_start(
+            out=gate_in[:].rearrange("p t h g -> p (t h) g"),
+            in_=gate_pre1.rearrange("t (h p) g -> p (t h) g", p=P),
+        )
+        gate_bias = keep.tile([P, T, G], BF16)
+        nc.scalar.dma_start(
+            out=gate_bias[:].rearrange("p t g -> p (t g)"),
+            in_=gb1.rearrange("t g -> (t g)").partition_broadcast(P),
+        )
+        bias_in = keep.tile([P, T + 1, V_TILES, E], BF16)
+        nc.scalar.dma_start(
+            out=bias_in[:, 0:T].rearrange("p m c e -> p (m c) e"),
+            in_=eb1.rearrange("t (c p) e -> p (t c) e", p=P),
+        )
+        nc.scalar.dma_start(out=bias_in[:, SHARED], in_=ebs1.rearrange("(c p) e -> p c e", p=P))
+
+        logits = keep.tile([P, T, B_TILES, G], F32)
+        nc.vector.tensor_tensor(
+            out=logits[:],
+            in0=gate_in[:],
+            in1=gate_bias[:].unsqueeze(2).to_broadcast([P, T, B_TILES, G]),
+            op=ALU.add,
+        )
+        rows_of_logits = logits[:].rearrange("p t h g -> p (t h) g")
+        top = keep.tile([P, T * B_TILES], F32)
+        nc.vector.tensor_reduce(out=top[:], in_=rows_of_logits, axis=AXIS.X, op=ALU.max)
+        nc.vector.tensor_tensor(
+            out=rows_of_logits,
+            in0=rows_of_logits,
+            in1=top[:].unsqueeze(2).to_broadcast([P, T * B_TILES, G]),
+            op=ALU.subtract,
+        )
+        gate = keep.tile([P, T, B_TILES, G], F32)
+        rows_of_gate = gate[:].rearrange("p t h g -> p (t h) g")
+        nc.scalar.activation(out=rows_of_gate, in_=rows_of_logits, func=ACT.Exp)
+        total = keep.tile([P, T * B_TILES], F32)
+        nc.vector.tensor_reduce(out=total[:], in_=rows_of_gate, axis=AXIS.X, op=ALU.add)
+        inverse = keep.tile([P, T * B_TILES], F32)
+        nc.vector.reciprocal(out=inverse[:], in_=total[:])
+        nc.vector.tensor_tensor(
+            out=rows_of_gate,
+            in0=rows_of_gate,
+            in1=inverse[:].unsqueeze(2).to_broadcast([P, T * B_TILES, G]),
+            op=ALU.mult,
+        )
+
+        bias = keep.tile([P, T + 1, V_TILES, E], F32)
+        nc.vector.tensor_copy(out=bias[:], in_=bias_in[:])
+
+        act_codes = keep.tile([P, T + 1, B], U32, align_bytes=64)
+        act_scales = keep.tile([P, T + 1, B], U8, align_bytes=64)
+        act_words = acts[:].bitcast(F32).rearrange("p (m h j w) -> p m h w j", m=T + 1, h=B_TILES, w=2)
+
+        def quantise_activations(m):
+            turned = psum.tile([P, 2, B], F32, tag="turned")
+            for h in range(B_TILES):
+                for w in range(2):
+                    nc.tensor.transpose(
+                        out=turned[:, w, h * P : (h + 1) * P], in_=act_words[:, m, h, w, :], identity=identity[:]
+                    )
+            side_by_side = stage.tile([P, B * PACK], BF16, align_bytes=64)
+            nc.vector.tensor_copy(
+                out=side_by_side[:].bitcast(F32).rearrange("p (b w) -> p b w", w=2),
+                in_=turned[:].rearrange("p w b -> p b w"),
+            )
+            nc.vector.quantize_mx(
+                out=act_codes[:, m, :].bitcast(FP8X4), scales=act_scales[:, m, :], in_=side_by_side[:]
+            )
+
+        def regroup(raw, half, vt, grouped):
+            units = slice(vt * P, (vt + 1) * P)
+            experts = slice(half * HALF, (half + 1) * HALF)
+            src = raw[:].rearrange("p t (v e) -> p t v e", e=E)[:, :, units, experts].rearrange("p t v e -> p v t e")
+            dst = grouped[:, :, units, :].rearrange("p e v t -> p v t e")
+            if (half * V_TILES + vt) % VECTOR_EVERY == 0:
+                nc.vector.tensor_copy(out=dst, in_=src)
+            else:
+                nc.scalar.copy(out=dst, in_=src)
+
+        def quantise(grouped, codes, scales):
+            for pair in range(HALF // 2):
+                cols = slice(pair * 2 * V, (pair + 1) * 2 * V)
+                nc.vector.quantize_mx(
+                    out=codes[:, cols].bitcast(FP8X4),
+                    scales=scales[:, cols],
+                    in_=grouped[:, 2 * pair : 2 * pair + 2].rearrange("p e v t -> p (e v t)"),
+                )
+
+        def multiply_and_relu(codes, scales, place, m, e):
+            hidden = relu_pool.tile([P, V_TILES, B], F32, tag="hidden")
+            for first in range(0, V_TILES, 2):
+                product = psum.tile([P, 2, B], F32, tag="product")
+                for s in range(2):
+                    cols = slice(place * V + (first + s) * P, place * V + (first + s + 1) * P)
+                    nc.tensor.matmul_mx(
+                        out=product[:, s, :],
+                        lhsT=codes[:, cols].bitcast(FP8X4),
+                        lhsT_scale=scales[:, cols],
+                        rhs=act_codes[:, m, :].bitcast(FP8X4),
+                        rhs_scale=act_scales[:, m, :],
+                        start=True,
+                        stop=True,
+                    )
+                for s in range(2):
+                    nc.scalar.activation(
+                        out=hidden[:, first + s, :],
+                        in_=product[:, s, :],
+                        func=ACT.Relu,
+                        bias=bias[:, m, first + s, e : e + 1],
+                        scale=1.0,
+                    )
+            return hidden
+
+        sums = keep.tile([P, T, B_TILES, V], F32)
+        terms = [0] * T
+
+        def turn_and_gate(hidden, takers):
+            turned = []
+            for h in range(B_TILES):
+                bank = psum.tile([P, V], F32, tag="turned", name="bank")
+                for vt in range(V_TILES):
+                    nc.tensor.transpose(
+                        out=bank[:, vt * P : (vt + 1) * P], in_=hidden[:, vt, h * P : (h + 1) * P], identity=identity[:]
+                    )
+                turned.append(bank)
+            for t, g in takers:
+                for h in range(B_TILES):
+                    if terms[t] == 0:
+                        nc.vector.tensor_scalar_mul(
+                            out=sums[:, t, h, :], in0=turned[h][:], scalar1=gate[:, t, h, g : g + 1]
+                        )
+                    else:
+                        nc.vector.scalar_tensor_tensor(
+                            out=sums[:, t, h, :],
+                            in0=turned[h][:],
+                            scalar=gate[:, t, h, g : g + 1],
+                            in1=sums[:, t, h, :],
+                            op0=ALU.mult,
+                            op1=ALU.add,
+                        )
+                terms[t] += 1
+                if terms[t] == G:
+                    nc.sync.dma_start(out=out[t].rearrange("(h p) v -> p h v", p=P), in_=sums[:, t])
+
+        quantise_activations(SHARED)
+
+        shared_codes = keep.tile([P, E * V], U32, align_bytes=64)
+        shared_scales = keep.tile([P, E * V], U8, align_bytes=64)
+        shared_grouped = []
+        for half in range(2):
+            grouped = grouped_pool.tile([P, HALF, V, PACK], BF16, tag="grouped", align_bytes=64)
+            shared_grouped.append(grouped)
+        for vt in range(V_TILES):
+            for half in range(2):
+                regroup(shared_raw, half, vt, shared_grouped[half])
+        for half in range(2):
+            cols = slice(half * HALF * V, (half + 1) * HALF * V)
+            quantise(shared_grouped[half], shared_codes[:, cols], shared_scales[:, cols])
+
+        for t in range(T):
+            quantise_activations(t)
+
+        def new_own_tiles():
+            grouped = grouped_pool.tile([P, HALF, V, PACK], BF16, tag="grouped", align_bytes=64)
+            codes = own_pool.tile([P, HALF * V], U32, tag="codes", align_bytes=64)
+            scales = own_pool.tile([P, HALF * V], U8, tag="scales", align_bytes=64)
+            return grouped, codes, scales
+
+        grouped, codes, scales = new_own_tiles()
+        for vt in range(V_TILES):
+            regroup(task_raw[0], 0, vt, grouped)
+        quantise(grouped, codes, scales)
+
+        waiting = None
+        for r in range(ROUNDS):
+            t, half = r // 2, r % 2
+            if half == 0 and t + 1 < T:
+                task_raw[t + 1] = load_matrix(ew1[t + 1])
+            if r + 1 < ROUNDS:
+                next_grouped, next_codes, next_scales = new_own_tiles()
+
+            for i in range(1 + HALF):
+                if i == 0:
+                    hidden = multiply_and_relu(shared_codes, shared_scales, r, SHARED, r)
+                    takers = [(task, E + r) for task in range(T)]
+                else:
+                    e = half * HALF + i - 1
+                    hidden = multiply_and_relu(codes, scales, i - 1, t, e)
+                    takers = [(t, e)]
+                if waiting is not None:
+                    turn_and_gate(waiting[0], waiting[1])
+                waiting = (hidden, takers)
+                if r + 1 < ROUNDS and i < V_TILES:
+                    regroup(task_raw[(r + 1) // 2], (r + 1) % 2, i, next_grouped)
+            if r + 1 < ROUNDS:
+                quantise(next_grouped, next_codes, next_scales)
+                codes, scales = next_codes, next_scales
+        turn_and_gate(waiting[0], waiting[1])

@@ -26,7 +26,8 @@ V_TILES = V // P
 HALF = E // 2
 ROUNDS = T * 2
 assert ROUNDS == E
-VECTOR_EVERY = 3
+ENGINES_AT_START = ("vector", "scalar", "gpsimd")
+ENGINES_IN_ROUNDS = ("scalar", "gpsimd")
 
 
 def tile_plelayer_pb_kernel(tc, task_h, share_h, ews1, ebs1, ew1, eb1, gate_pre1, gb1, out):
@@ -131,15 +132,17 @@ def tile_plelayer_pb_kernel(tc, task_h, share_h, ews1, ebs1, ew1, eb1, gate_pre1
                 out=act_codes[:, m, :].bitcast(FP8X4), scales=act_scales[:, m, :], in_=side_by_side[:]
             )
 
-        def regroup(raw, half, vt, grouped):
+        def regroup(raw, half, vt, grouped, engine):
             units = slice(vt * P, (vt + 1) * P)
             experts = slice(half * HALF, (half + 1) * HALF)
             src = raw[:].rearrange("p t (v e) -> p t v e", e=E)[:, :, units, experts].rearrange("p t v e -> p v t e")
             dst = grouped[:, :, units, :].rearrange("p e v t -> p v t e")
-            if (half * V_TILES + vt) % VECTOR_EVERY == 0:
+            if engine == "vector":
                 nc.vector.tensor_copy(out=dst, in_=src)
-            else:
+            elif engine == "scalar":
                 nc.scalar.copy(out=dst, in_=src)
+            else:
+                nc.gpsimd.tensor_scalar(out=dst, in0=src, scalar1=1.0, scalar2=0.0, op0=ALU.mult, op1=ALU.add)
 
         def quantise(grouped, codes, scales):
             for pair in range(HALF // 2):
@@ -190,8 +193,8 @@ def tile_plelayer_pb_kernel(tc, task_h, share_h, ews1, ebs1, ew1, eb1, gate_pre1
             for t, g in takers:
                 for h in range(B_TILES):
                     if terms[t] == 0:
-                        nc.vector.tensor_scalar_mul(
-                            out=sums[:, t, h, :], in0=turned[h][:], scalar1=gate[:, t, h, g : g + 1]
+                        nc.scalar.activation(
+                            out=sums[:, t, h, :], in_=turned[h][:], func=ACT.Copy, scale=gate[:, t, h, g : g + 1]
                         )
                     else:
                         nc.vector.scalar_tensor_tensor(
@@ -214,9 +217,11 @@ def tile_plelayer_pb_kernel(tc, task_h, share_h, ews1, ebs1, ew1, eb1, gate_pre1
         for half in range(2):
             grouped = grouped_pool.tile([P, HALF, V, PACK], BF16, tag="grouped", align_bytes=64)
             shared_grouped.append(grouped)
+        copies = 0
         for vt in range(V_TILES):
             for half in range(2):
-                regroup(shared_raw, half, vt, shared_grouped[half])
+                regroup(shared_raw, half, vt, shared_grouped[half], ENGINES_AT_START[copies % len(ENGINES_AT_START)])
+                copies += 1
         for half in range(2):
             cols = slice(half * HALF * V, (half + 1) * HALF * V)
             quantise(shared_grouped[half], shared_codes[:, cols], shared_scales[:, cols])
@@ -232,7 +237,8 @@ def tile_plelayer_pb_kernel(tc, task_h, share_h, ews1, ebs1, ew1, eb1, gate_pre1
 
         grouped, codes, scales = new_own_tiles()
         for vt in range(V_TILES):
-            regroup(task_raw[0], 0, vt, grouped)
+            regroup(task_raw[0], 0, vt, grouped, ENGINES_AT_START[copies % len(ENGINES_AT_START)])
+            copies += 1
         quantise(grouped, codes, scales)
 
         waiting = None
@@ -255,7 +261,9 @@ def tile_plelayer_pb_kernel(tc, task_h, share_h, ews1, ebs1, ew1, eb1, gate_pre1
                     turn_and_gate(waiting[0], waiting[1])
                 waiting = (hidden, takers)
                 if r + 1 < ROUNDS and i < V_TILES:
-                    regroup(task_raw[(r + 1) // 2], (r + 1) % 2, i, next_grouped)
+                    engine = ENGINES_IN_ROUNDS[copies % len(ENGINES_IN_ROUNDS)]
+                    regroup(task_raw[(r + 1) // 2], (r + 1) % 2, i, next_grouped, engine)
+                    copies += 1
             if r + 1 < ROUNDS:
                 quantise(next_grouped, next_codes, next_scales)
                 codes, scales = next_codes, next_scales

@@ -26,8 +26,8 @@ V_TILES = V // P
 HALF = E // 2
 ROUNDS = T * 2
 assert ROUNDS == E
-ENGINES_AT_START = ("vector", "scalar", "gpsimd")
-ENGINES_IN_ROUNDS = ("scalar", "gpsimd")
+ENGINES_AT_START = ("vector", "vector", "scalar")
+ENGINES_IN_ROUNDS = ("scalar", "gpsimd", "gpsimd")
 
 
 def tile_plelayer_pb_kernel(tc, task_h, share_h, ews1, ebs1, ew1, eb1, gate_pre1, gb1, out):

@@ -18,125 +18,213 @@ FLOPS = 2 * (T + 1) * B * U * V * E
 
 P = 128
 PACK = 4
-assert U == P * PACK
-
 SHARED = T
 B_TILES = B // P
-V_TILES = V // P
+
+UNITS = P // E
+STEP_TILES = 4
+STEP_COLS = STEP_TILES * P
+STEPS = V * E // STEP_COLS
+ALL_STEPS = T * STEPS
+CHUNK_COLS = 2 * STEP_COLS
+TILES = V * E // P
+RELU_STEP = STEPS - 1
+BIAS_TILES = RELU_STEP * STEP_TILES
+
 HALF = E // 2
-ROUNDS = T * 2
-assert ROUNDS == E
-ENGINES_AT_START = ("vector", "vector", "scalar")
-ENGINES_IN_ROUNDS = ("scalar", "gpsimd", "gpsimd")
+V_TILES = V // P
+OWN_ENGINES = ("vector", "scalar")
+SHARED_ENGINES = ("scalar", "vector")
+QB = 32
+Q = B // QB
 
 
 def tile_plelayer_pb_kernel(tc, task_h, share_h, ews1, ebs1, ew1, eb1, gate_pre1, gb1, out):
     nc = tc.nc
     with ExitStack() as stack:
         keep = stack.enter_context(tc.tile_pool(name="keep", bufs=1))
-        stage = stack.enter_context(tc.tile_pool(name="stage", bufs=2))
-        raw_pool = stack.enter_context(tc.tile_pool(name="raw", bufs=2))
-        grouped_pool = stack.enter_context(tc.tile_pool(name="grouped", bufs=2))
-        own_pool = stack.enter_context(tc.tile_pool(name="own", bufs=3))
-        relu_pool = stack.enter_context(tc.tile_pool(name="relu", bufs=3))
-        psum = stack.enter_context(tc.psum_pool(name="psum", bufs=4))
+        raw_pool = stack.enter_context(tc.tile_pool(name="raw", bufs=8))
+        grouped_pool = stack.enter_context(tc.tile_pool(name="grouped", bufs=6))
+        codes_pool = stack.enter_context(tc.tile_pool(name="codes", bufs=6))
+        work = stack.enter_context(tc.tile_pool(name="work", bufs=2))
+        gated_pool = stack.enter_context(tc.tile_pool(name="gated", bufs=3))
+        product_pool = stack.enter_context(tc.psum_pool(name="product", bufs=4))
+        turned_pool = stack.enter_context(tc.psum_pool(name="turned", bufs=2))
+        sums_pool = stack.enter_context(tc.psum_pool(name="sums", bufs=2))
+        stack.enter_context(tc.manual_schedule())
 
         identity = keep.tile([P, P], F32)
         make_identity(nc, identity[:])
 
-        def load_matrix(weights):
-            raw = raw_pool.tile([P, PACK, V * E], BF16, tag="raw")
-            rows = weights.rearrange("(p t) v e -> p t (v e)", t=PACK)
-            for vt in range(V_TILES):
-                cols = slice(vt * P * E, (vt + 1) * P * E)
-                nc.sync.dma_start(out=raw[:, :, cols], in_=rows[:, :, cols])
+        acts = keep.tile([P, T + 1, B_TILES, U], BF16)
+
+        def load_acts(m):
+            src = share_h if m == SHARED else task_h[m]
+            nc.sync.dma_start(out=acts[:, m], in_=src.rearrange("(h p) u -> p h u", p=P))
+
+        def load_chunk(weights, c):
+            raw = raw_pool.tile([P, PACK, CHUNK_COLS], BF16, tag="raw")
+            rows = weights.rearrange("(p f) v e -> p f (v e)", f=PACK)
+            nc.sync.dma_start(out=raw[:], in_=rows[:, :, c * CHUNK_COLS : (c + 1) * CHUNK_COLS])
             return raw
 
-        acts = keep.tile([P, (T + 1) * B_TILES * U], BF16)
-        acts_by_stream = acts[:].rearrange("p (m h u) -> p m h u", m=T + 1, h=B_TILES)
-        nc.sync.dma_start(out=acts_by_stream[:, SHARED], in_=share_h.rearrange("(h p) u -> p h u", p=P))
-        shared_raw = load_matrix(ews1)
-        nc.sync.dma_start(
-            out=acts_by_stream[:, 0:T].rearrange("p m h u -> p (m h) u"),
-            in_=task_h.rearrange("t (h p) u -> p (t h) u", p=P),
-        )
-        task_raw = {0: load_matrix(ew1[0])}
-
-        gate_in = keep.tile([P, T, B_TILES, G], BF16)
-        nc.scalar.dma_start(
-            out=gate_in[:].rearrange("p t h g -> p (t h) g"),
-            in_=gate_pre1.rearrange("t (h p) g -> p (t h) g", p=P),
-        )
+        gate_in = keep.tile([P, T * B_TILES, G], BF16)
+        nc.scalar.dma_start(out=gate_in[:], in_=gate_pre1.rearrange("t (h p) g -> p (t h) g", p=P))
         gate_bias = keep.tile([P, T, G], BF16)
         nc.scalar.dma_start(
             out=gate_bias[:].rearrange("p t g -> p (t g)"),
             in_=gb1.rearrange("t g -> (t g)").partition_broadcast(P),
         )
-        bias_in = keep.tile([P, T + 1, V_TILES, E], BF16)
-        nc.scalar.dma_start(
-            out=bias_in[:, 0:T].rearrange("p m c e -> p (m c) e"),
-            in_=eb1.rearrange("t (c p) e -> p (t c) e", p=P),
-        )
-        nc.scalar.dma_start(out=bias_in[:, SHARED], in_=ebs1.rearrange("(c p) e -> p c e", p=P))
+        bias_rows = keep.tile([P, P], BF16)
+        nc.scalar.dma_start(out=bias_rows[:], in_=eb1.rearrange("t (j x) e -> (t j) (x e)", x=UNITS))
+        gate_in2 = keep.tile([P, T * Q, G], BF16)
+        for r in range(HALF):
+            nc.scalar.dma_start(
+                out=gate_in2[r * QB : (r + 1) * QB], in_=gate_pre1.rearrange("t (q b) g -> b (t q) g", b=QB)
+            )
+        shared_bias_in = keep.tile([P, V_TILES, E], BF16)
+        nc.scalar.dma_start(out=shared_bias_in[:], in_=ebs1.rearrange("(c p) e -> p c e", p=P))
 
-        logits = keep.tile([P, T, B_TILES, G], F32)
-        nc.vector.tensor_tensor(
-            out=logits[:],
-            in0=gate_in[:],
-            in1=gate_bias[:].unsqueeze(2).to_broadcast([P, T, B_TILES, G]),
-            op=ALU.add,
-        )
-        rows_of_logits = logits[:].rearrange("p t h g -> p (t h) g")
-        top = keep.tile([P, T * B_TILES], F32)
-        nc.vector.tensor_reduce(out=top[:], in_=rows_of_logits, axis=AXIS.X, op=ALU.max)
-        nc.vector.tensor_tensor(
-            out=rows_of_logits,
-            in0=rows_of_logits,
-            in1=top[:].unsqueeze(2).to_broadcast([P, T * B_TILES, G]),
-            op=ALU.subtract,
-        )
-        gate = keep.tile([P, T, B_TILES, G], F32)
-        rows_of_gate = gate[:].rearrange("p t h g -> p (t h) g")
-        nc.scalar.activation(out=rows_of_gate, in_=rows_of_logits, func=ACT.Exp)
-        total = keep.tile([P, T * B_TILES], F32)
-        nc.vector.tensor_reduce(out=total[:], in_=rows_of_gate, axis=AXIS.X, op=ALU.add)
-        inverse = keep.tile([P, T * B_TILES], F32)
-        nc.vector.reciprocal(out=inverse[:], in_=total[:])
-        nc.vector.tensor_tensor(
-            out=rows_of_gate,
-            in0=rows_of_gate,
-            in1=inverse[:].unsqueeze(2).to_broadcast([P, T * B_TILES, G]),
-            op=ALU.mult,
-        )
+        load_acts(0)
+        own_raw, shared_raw = {}, {}
+        own_raw[0] = load_chunk(ew1[0], 0)
+        load_acts(SHARED)
+        shared_raw[0] = load_chunk(ews1, 0)
+        for c in range(1, V_TILES):
+            own_raw[c] = load_chunk(ew1[0], c)
+            shared_raw[c] = load_chunk(ews1, c)
+        for t in range(1, T):
+            load_acts(t)
 
-        bias = keep.tile([P, T + 1, V_TILES, E], F32)
-        nc.vector.tensor_copy(out=bias[:], in_=bias_in[:])
+        select = keep.tile([P, UNITS], F32)
+        nc.vector.tensor_reduce(
+            out=select[:], in_=identity[:].rearrange("p (v e) -> p v e", e=E), axis=AXIS.X, op=ALU.add
+        )
+        bias_f32 = keep.tile([P, P], F32)
+        nc.vector.tensor_copy(out=bias_f32[:], in_=bias_rows[:])
+        bias_bank = turned_pool.tile([P, P], F32, tag="turned")
+        nc.tensor.transpose(out=bias_bank[:], in_=bias_f32[:], identity=identity[:])
+        bias = keep.tile([P, T, TILES], F32)
+        nc.vector.tensor_copy(out=bias[:].rearrange("p t j -> p (t j)"), in_=bias_bank[:])
+        minus_bias = keep.tile([P, T, TILES], F32)
+        nc.vector.tensor_scalar(out=minus_bias[:], in0=bias[:], scalar1=-1.0, scalar2=None, op0=ALU.mult)
+
+        def softmax_numerators(logits_in, blocks, name):
+            logits = keep.tile([P, T * blocks, G], F32, name="logits_" + name)
+            nc.vector.tensor_tensor(
+                out=logits[:].rearrange("p (t q) g -> p t q g", t=T),
+                in0=logits_in[:].rearrange("p (t q) g -> p t q g", t=T),
+                in1=gate_bias[:].unsqueeze(2).to_broadcast([P, T, blocks, G]),
+                op=ALU.add,
+            )
+            top = keep.tile([P, T * blocks], F32, name="top_" + name)
+            nc.vector.tensor_reduce(out=top[:], in_=logits[:], axis=AXIS.X, op=ALU.max)
+            nc.vector.tensor_tensor(
+                out=logits[:], in0=logits[:], in1=top[:].unsqueeze(2).to_broadcast([P, T * blocks, G]), op=ALU.subtract
+            )
+            powers = keep.tile([P, T * blocks, G], F32, name="powers_" + name)
+            nc.scalar.activation(out=powers[:], in_=logits[:], func=ACT.Exp)
+            total = keep.tile([P, T * blocks], F32, name="total_" + name)
+            nc.vector.tensor_reduce(out=total[:], in_=powers[:], axis=AXIS.X, op=ALU.add)
+            inverse = keep.tile([P, T * blocks], F32, name="inverse_" + name)
+            nc.vector.reciprocal(out=inverse[:], in_=total[:])
+            return powers, inverse
+
+        gate_of_column = keep.tile([P, T, B], F32)
+
+        def make_own_gates():
+            powers, inverse = softmax_numerators(gate_in, B_TILES, "own")
+            gates = keep.tile([P, T * B_TILES, E], F32)
+            nc.vector.tensor_tensor(
+                out=gates[:],
+                in0=powers[:, :, 0:E],
+                in1=inverse[:].unsqueeze(2).to_broadcast([P, T * B_TILES, E]),
+                op=ALU.mult,
+            )
+            spread = keep.tile([P, T * B_TILES, UNITS, E], F32)
+            nc.vector.tensor_copy(
+                out=spread[:], in_=gates[:].unsqueeze(2).to_broadcast([P, T * B_TILES, UNITS, E])
+            )
+            for pair in range(T // 2):
+                bank = turned_pool.tile([P, 2 * B], F32, tag="turned")
+                for i in range(2 * B_TILES):
+                    nc.tensor.transpose(
+                        out=bank[:, i * P : (i + 1) * P],
+                        in_=spread[:, pair * 2 * B_TILES + i].rearrange("p v e -> p (v e)"),
+                        identity=identity[:],
+                    )
+                nc.scalar.copy(
+                    out=gate_of_column[:, 2 * pair : 2 * pair + 2].rearrange("p t b -> p (t b)"), in_=bank[:]
+                )
+
+        bias_moving = keep.tile([P, T, BIAS_TILES, UNITS], F32)
+
+        def make_bias_moving(first, last, engine):
+            shape = [P, last - first, BIAS_TILES, UNITS]
+            engine.tensor_tensor(
+                out=bias_moving[:, first:last],
+                in0=bias[:, first:last, 0:BIAS_TILES].unsqueeze(3).to_broadcast(shape),
+                in1=select[:].unsqueeze(1).unsqueeze(1).to_broadcast(shape),
+                op=ALU.mult,
+            )
+
+        block_gates = keep.tile([P, 2, Q, T, QB], F32)
+        shared_bias = keep.tile([P, V_TILES, E], F32)
+
+        def make_shared_gates():
+            nc.vector.tensor_copy(out=shared_bias[:], in_=shared_bias_in[:])
+            same_sample = keep.tile([P, QB], F32)
+            nc.vector.tensor_reduce(
+                out=same_sample[:], in_=identity[:].rearrange("p (r b) -> p b r", b=QB), axis=AXIS.X, op=ALU.add
+            )
+            own_copy = keep.tile([P, HALF], F32)
+            nc.vector.tensor_reduce(
+                out=own_copy[:], in_=identity[:].rearrange("p (r b) -> p r b", b=QB), axis=AXIS.X, op=ALU.add
+            )
+            powers, inverse = softmax_numerators(gate_in2, Q, "shared")
+            picked = keep.tile([P, T * Q, 2, HALF], F32)
+            nc.vector.tensor_tensor(
+                out=picked[:],
+                in0=powers[:, :, E:G].rearrange("p x (s e) -> p x s e", e=HALF),
+                in1=own_copy[:].unsqueeze(1).unsqueeze(1).to_broadcast([P, T * Q, 2, HALF]),
+                op=ALU.mult,
+            )
+            mine = keep.tile([P, T * Q, 2], F32)
+            nc.vector.tensor_reduce(out=mine[:], in_=picked[:], axis=AXIS.X, op=ALU.add)
+            nc.vector.tensor_tensor(
+                out=mine[:], in0=mine[:], in1=inverse[:].unsqueeze(2).to_broadcast([P, T * Q, 2]), op=ALU.mult
+            )
+            for s in range(2):
+                nc.vector.tensor_tensor(
+                    out=block_gates[:, s],
+                    in0=mine[:, :, s].rearrange("p (t q) -> p q t", t=T).unsqueeze(3).to_broadcast([P, Q, T, QB]),
+                    in1=same_sample[:].unsqueeze(1).unsqueeze(1).to_broadcast([P, Q, T, QB]),
+                    op=ALU.mult,
+                )
 
         act_codes = keep.tile([P, T + 1, B], U32, align_bytes=64)
         act_scales = keep.tile([P, T + 1, B], U8, align_bytes=64)
-        act_words = acts[:].bitcast(F32).rearrange("p (m h j w) -> p m h w j", m=T + 1, h=B_TILES, w=2)
+        act_words = acts[:].rearrange("p m h u -> p (m h u)").bitcast(F32).rearrange(
+            "p (m h j w) -> p m h w j", m=T + 1, h=B_TILES, w=2
+        )
 
         def quantise_activations(m):
-            turned = psum.tile([P, 2, B], F32, tag="turned")
+            bank = turned_pool.tile([P, 2, B], F32, tag="turned")
             for h in range(B_TILES):
                 for w in range(2):
                     nc.tensor.transpose(
-                        out=turned[:, w, h * P : (h + 1) * P], in_=act_words[:, m, h, w, :], identity=identity[:]
+                        out=bank[:, w, h * P : (h + 1) * P], in_=act_words[:, m, h, w, :], identity=identity[:]
                     )
-            side_by_side = stage.tile([P, B * PACK], BF16, align_bytes=64)
+            side_by_side = work.tile([P, B * PACK], BF16, align_bytes=64)
             nc.vector.tensor_copy(
                 out=side_by_side[:].bitcast(F32).rearrange("p (b w) -> p b w", w=2),
-                in_=turned[:].rearrange("p w b -> p b w"),
+                in_=bank[:].rearrange("p w b -> p b w"),
             )
             nc.vector.quantize_mx(
                 out=act_codes[:, m, :].bitcast(FP8X4), scales=act_scales[:, m, :], in_=side_by_side[:]
             )
 
-        def regroup(raw, half, vt, grouped, engine):
-            units = slice(vt * P, (vt + 1) * P)
-            experts = slice(half * HALF, (half + 1) * HALF)
-            src = raw[:].rearrange("p t (v e) -> p t v e", e=E)[:, :, units, experts].rearrange("p t v e -> p v t e")
-            dst = grouped[:, :, units, :].rearrange("p e v t -> p v t e")
+        def copy(dst, src, engine):
             if engine == "vector":
                 nc.vector.tensor_copy(out=dst, in_=src)
             elif engine == "scalar":
@@ -144,23 +232,21 @@ def tile_plelayer_pb_kernel(tc, task_h, share_h, ews1, ebs1, ew1, eb1, gate_pre1
             else:
                 nc.gpsimd.tensor_scalar(out=dst, in0=src, scalar1=1.0, scalar2=0.0, op0=ALU.mult, op1=ALU.add)
 
-        def quantise(grouped, codes, scales):
-            for pair in range(HALF // 2):
-                cols = slice(pair * 2 * V, (pair + 1) * 2 * V)
-                nc.vector.quantize_mx(
-                    out=codes[:, cols].bitcast(FP8X4),
-                    scales=scales[:, cols],
-                    in_=grouped[:, 2 * pair : 2 * pair + 2].rearrange("p e v t -> p (e v t)"),
-                )
+        def quantise(grouped):
+            codes = codes_pool.tile([P, STEP_COLS], U32, tag="codes", align_bytes=64)
+            scales = codes_pool.tile([P, STEP_COLS], U8, tag="scales", align_bytes=64)
+            nc.vector.quantize_mx(out=codes[:].bitcast(FP8X4), scales=scales[:], in_=grouped)
+            return codes, scales
 
-        def multiply_and_relu(codes, scales, place, m, e):
-            hidden = relu_pool.tile([P, V_TILES, B], F32, tag="hidden")
-            for first in range(0, V_TILES, 2):
-                product = psum.tile([P, 2, B], F32, tag="product")
+        def multiply(weights, m):
+            codes, scales = weights
+            banks = []
+            for first in range(0, STEP_TILES, 2):
+                bank = product_pool.tile([P, 2, B], F32, tag="product")
                 for s in range(2):
-                    cols = slice(place * V + (first + s) * P, place * V + (first + s + 1) * P)
+                    cols = slice((first + s) * P, (first + s + 1) * P)
                     nc.tensor.matmul_mx(
-                        out=product[:, s, :],
+                        out=bank[:, s, :],
                         lhsT=codes[:, cols].bitcast(FP8X4),
                         lhsT_scale=scales[:, cols],
                         rhs=act_codes[:, m, :].bitcast(FP8X4),
@@ -168,103 +254,220 @@ def tile_plelayer_pb_kernel(tc, task_h, share_h, ews1, ebs1, ew1, eb1, gate_pre1
                         start=True,
                         stop=True,
                     )
-                for s in range(2):
+                banks.append(bank)
+            return banks
+
+        own_grouped, own_weights, own_banks, own_gated = {}, {}, {}, {}
+
+        def own_copy_in(k):
+            grouped = grouped_pool.tile([P, STEP_COLS, PACK], BF16, tag="grouped", align_bytes=64)
+            cols = slice((k % 2) * STEP_COLS, (k % 2 + 1) * STEP_COLS)
+            copy(grouped[:], own_raw[k // 2][:, :, cols].rearrange("p f c -> p c f"), OWN_ENGINES[k % len(OWN_ENGINES)])
+            own_grouped[k] = grouped
+
+        def own_quantise(k):
+            own_weights[k] = quantise(own_grouped[k][:].rearrange("p c f -> p (c f)"))
+
+        def own_multiply(k):
+            own_banks[k] = multiply(own_weights[k], k // STEPS)
+
+        def own_gate(k):
+            t, step = k // STEPS, k % STEPS
+            gated = gated_pool.tile([P, STEP_TILES, B], F32, tag="gated")
+            if step == RELU_STEP:
+                relu = work.tile([P, STEP_TILES, B], F32, tag="relu")
+                for i in range(STEP_TILES):
+                    j = step * STEP_TILES + i
                     nc.scalar.activation(
-                        out=hidden[:, first + s, :],
-                        in_=product[:, s, :],
+                        out=relu[:, i, :],
+                        in_=own_banks[k][i // 2][:, i % 2, :],
                         func=ACT.Relu,
-                        bias=bias[:, m, first + s, e : e + 1],
+                        bias=bias[:, t, j : j + 1],
                         scale=1.0,
                     )
-            return hidden
-
-        sums = keep.tile([P, T, B_TILES, V], F32)
-        terms = [0] * T
-
-        def turn_and_gate(hidden, takers):
-            turned = []
-            for h in range(B_TILES):
-                bank = psum.tile([P, V], F32, tag="turned", name="bank")
-                for vt in range(V_TILES):
-                    nc.tensor.transpose(
-                        out=bank[:, vt * P : (vt + 1) * P], in_=hidden[:, vt, h * P : (h + 1) * P], identity=identity[:]
+                nc.vector.tensor_tensor(
+                    out=gated[:],
+                    in0=relu[:],
+                    in1=gate_of_column[:, t, :].unsqueeze(1).to_broadcast([P, STEP_TILES, B]),
+                    op=ALU.mult,
+                )
+            else:
+                for i in range(STEP_TILES):
+                    j = step * STEP_TILES + i
+                    nc.vector.scalar_tensor_tensor(
+                        out=gated[:, i, :],
+                        in0=own_banks[k][i // 2][:, i % 2, :],
+                        scalar=minus_bias[:, t, j : j + 1],
+                        in1=gate_of_column[:, t, :],
+                        op0=ALU.max,
+                        op1=ALU.mult,
                     )
-                turned.append(bank)
-            for t, g in takers:
+            own_gated[k] = gated
+
+        sums = {}
+
+        def own_add(k):
+            t, step = k // STEPS, k % STEPS
+            if step == 0:
                 for h in range(B_TILES):
-                    if terms[t] == 0:
-                        nc.scalar.activation(
-                            out=sums[:, t, h, :], in_=turned[h][:], func=ACT.Copy, scale=gate[:, t, h, g : g + 1]
-                        )
-                    else:
-                        nc.vector.scalar_tensor_tensor(
-                            out=sums[:, t, h, :],
-                            in0=turned[h][:],
-                            scalar=gate[:, t, h, g : g + 1],
-                            in1=sums[:, t, h, :],
-                            op0=ALU.mult,
-                            op1=ALU.add,
-                        )
-                terms[t] += 1
-                if terms[t] == G:
-                    nc.sync.dma_start(out=out[t].rearrange("(h p) v -> p h v", p=P), in_=sums[:, t])
+                    bank = sums_pool.tile([P, V], F32, tag="sums", name="sum_bank")
+                    nc.tensor.matmul(
+                        out=bank[:, 0 : BIAS_TILES * UNITS],
+                        lhsT=gate_of_column[:, t, h * P : (h + 1) * P],
+                        rhs=bias_moving[:, t].rearrange("p j v -> p (j v)"),
+                        start=True,
+                        stop=False,
+                    )
+                    sums[t, h] = bank
+            for i in range(STEP_TILES):
+                j = step * STEP_TILES + i
+                for h in range(B_TILES):
+                    nc.tensor.matmul(
+                        out=sums[t, h][:, j * UNITS : (j + 1) * UNITS],
+                        lhsT=own_gated[k][:, i, h * P : (h + 1) * P],
+                        rhs=select[:],
+                        start=False,
+                        stop=(j == TILES - 1),
+                    )
 
-        quantise_activations(SHARED)
+        shared_grouped, shared_hidden = {}, {}
+        hidden_by_sample = keep.tile([P, 2, Q, V], F32)
 
-        shared_codes = keep.tile([P, E * V], U32, align_bytes=64)
-        shared_scales = keep.tile([P, E * V], U8, align_bytes=64)
-        shared_grouped = []
-        for half in range(2):
-            grouped = grouped_pool.tile([P, HALF, V, PACK], BF16, tag="grouped", align_bytes=64)
-            shared_grouped.append(grouped)
-        copies = 0
-        for vt in range(V_TILES):
-            for half in range(2):
-                regroup(shared_raw, half, vt, shared_grouped[half], ENGINES_AT_START[copies % len(ENGINES_AT_START)])
-                copies += 1
-        for half in range(2):
-            cols = slice(half * HALF * V, (half + 1) * HALF * V)
-            quantise(shared_grouped[half], shared_codes[:, cols], shared_scales[:, cols])
+        def shared_copy_in(i):
+            vt, s = i // 2, i % 2
+            grouped = grouped_pool.tile([P, HALF, P, PACK], BF16, tag="grouped", align_bytes=64)
+            src = shared_raw[vt][:].rearrange("p f (v e) -> p f v e", e=E)[:, :, :, s * HALF : (s + 1) * HALF]
+            copy(
+                grouped[:].rearrange("p e v f -> p v f e"),
+                src.rearrange("p f v e -> p v f e"),
+                SHARED_ENGINES[i % len(SHARED_ENGINES)],
+            )
+            shared_grouped[i] = grouped
 
-        for t in range(T):
-            quantise_activations(t)
+        def shared_multiply(i):
+            vt, s = i // 2, i % 2
+            weights = quantise(shared_grouped[i][:].rearrange("p e v f -> p (e v f)"))
+            banks = multiply(weights, SHARED)
+            hidden = work.tile([P, Q, HALF, QB], F32, tag="hidden")
+            for e in range(HALF):
+                nc.scalar.activation(
+                    out=hidden[:, :, e, :],
+                    in_=banks[e // 2][:, e % 2, :].rearrange("p (q b) -> p q b", b=QB),
+                    func=ACT.Relu,
+                    bias=shared_bias[:, vt, s * HALF + e : s * HALF + e + 1],
+                    scale=1.0,
+                )
+            shared_hidden[i] = hidden
 
-        def new_own_tiles():
-            grouped = grouped_pool.tile([P, HALF, V, PACK], BF16, tag="grouped", align_bytes=64)
-            codes = own_pool.tile([P, HALF * V], U32, tag="codes", align_bytes=64)
-            scales = own_pool.tile([P, HALF * V], U8, tag="scales", align_bytes=64)
-            return grouped, codes, scales
-
-        grouped, codes, scales = new_own_tiles()
-        for vt in range(V_TILES):
-            regroup(task_raw[0], 0, vt, grouped, ENGINES_AT_START[copies % len(ENGINES_AT_START)])
-            copies += 1
-        quantise(grouped, codes, scales)
-
-        waiting = None
-        for r in range(ROUNDS):
-            t, half = r // 2, r % 2
-            if half == 0 and t + 1 < T:
-                task_raw[t + 1] = load_matrix(ew1[t + 1])
-            if r + 1 < ROUNDS:
-                next_grouped, next_codes, next_scales = new_own_tiles()
-
-            for i in range(1 + HALF):
-                if i == 0:
-                    hidden = multiply_and_relu(shared_codes, shared_scales, r, SHARED, r)
-                    takers = [(task, E + r) for task in range(T)]
+        def shared_turn(i):
+            vt, s = i // 2, i % 2
+            for first in range(0, Q, 4):
+                bank = turned_pool.tile([P, 4, P], F32, tag="turned")
+                for q in range(4):
+                    nc.tensor.transpose(
+                        out=bank[:, q, :],
+                        in_=shared_hidden[i][:, first + q].rearrange("p e b -> p (e b)"),
+                        identity=identity[:],
+                    )
+                dst = hidden_by_sample[:, s, first : first + 4, vt * P : (vt + 1) * P]
+                if first == 0:
+                    nc.vector.tensor_copy(out=dst, in_=bank[:])
                 else:
-                    e = half * HALF + i - 1
-                    hidden = multiply_and_relu(codes, scales, i - 1, t, e)
-                    takers = [(t, e)]
-                if waiting is not None:
-                    turn_and_gate(waiting[0], waiting[1])
-                waiting = (hidden, takers)
-                if r + 1 < ROUNDS and i < V_TILES:
-                    engine = ENGINES_IN_ROUNDS[copies % len(ENGINES_IN_ROUNDS)]
-                    regroup(task_raw[(r + 1) // 2], (r + 1) % 2, i, next_grouped, engine)
-                    copies += 1
-            if r + 1 < ROUNDS:
-                quantise(next_grouped, next_codes, next_scales)
-                codes, scales = next_codes, next_scales
-        turn_and_gate(waiting[0], waiting[1])
+                    nc.scalar.copy(out=dst, in_=bank[:])
+
+        shared_sum = {}
+
+        def shared_gate(q):
+            bank = turned_pool.tile([P, V], F32, tag="turned")
+            for s in range(2):
+                nc.tensor.matmul(
+                    out=bank[:],
+                    lhsT=block_gates[:, s, q].rearrange("p t b -> p (t b)"),
+                    rhs=hidden_by_sample[:, s, q, :],
+                    start=(s == 0),
+                    stop=(s == 1),
+                )
+            if q % 2 == 0:
+                shared_sum[q // 2] = work.tile([P, 2, V], F32, tag="shared_sum", name="shared_sum")
+            nc.scalar.copy(out=shared_sum[q // 2][:, q % 2, :], in_=bank[:])
+            if q % 2 == 1:
+                for t in range(T):
+                    nc.sync.dma_start(
+                        out=out[t].rearrange("(q b) v -> b q v", b=QB)[:, q - 1 : q + 1, :],
+                        in_=shared_sum[q // 2][t * QB : (t + 1) * QB],
+                    )
+
+        shared_part = {}
+
+        def load_shared_part(t):
+            part = work.tile([P, B_TILES, V], F32, tag="hidden", name="part")
+            nc.sync.dma_start(out=part[:], in_=out[t].rearrange("(h p) v -> p h v", p=P))
+            shared_part[t] = part
+
+        own_part = {}
+
+        def hold_own_part(t):
+            own = work.tile([P, B_TILES, V], F32, tag="own", name="own")
+            for h in range(B_TILES):
+                nc.scalar.copy(out=own[:, h, :], in_=sums[t, h][:])
+            own_part[t] = own
+
+        def finish(t):
+            result = work.tile([P, B_TILES, V], F32, tag="relu", name="result")
+            if t in own_part:
+                nc.gpsimd.tensor_tensor(out=result[:], in0=own_part[t][:], in1=shared_part[t][:], op=ALU.add)
+            else:
+                for h in range(B_TILES):
+                    nc.vector.tensor_tensor(
+                        out=result[:, h, :], in0=sums[t, h][:], in1=shared_part[t][:, h, :], op=ALU.add
+                    )
+            nc.sync.dma_start(out=out[t].rearrange("(h p) v -> p h v", p=P), in_=result[:])
+
+        LEAD = 3
+        quantise_activations(0)
+        for slot in range(-LEAD, ALL_STEPS + 1):
+            k = slot
+            if 0 <= k + LEAD < ALL_STEPS:
+                own_copy_in(k + LEAD)
+            if 0 <= slot + 1 < 2 * V_TILES:
+                shared_copy_in(slot + 1)
+            if slot == -LEAD:
+                make_own_gates()
+                make_bias_moving(0, 1, nc.vector)
+                quantise_activations(SHARED)
+            if slot == -1:
+                make_shared_gates()
+                make_bias_moving(1, T, nc.gpsimd)
+            if 0 <= k + 2 < ALL_STEPS:
+                own_quantise(k + 2)
+            if 0 <= k + 1 < ALL_STEPS:
+                own_multiply(k + 1)
+            if 0 <= k < ALL_STEPS:
+                own_gate(k)
+            if 0 <= k - 1 < ALL_STEPS:
+                own_add(k - 1)
+            if 0 <= slot < 2 * V_TILES:
+                shared_multiply(slot)
+            if 0 <= slot - 1 < 2 * V_TILES:
+                shared_turn(slot - 1)
+            if slot % 2 == 0 and 0 <= slot < (T - 1) * 8:
+                c = V_TILES + slot // 2
+                if c < T * V_TILES:
+                    own_raw[c] = load_chunk(ew1[c // V_TILES], c % V_TILES)
+            if slot in (2, 4, 6):
+                quantise_activations(slot // 2)
+            if k - 1 == STEPS - 1 or k - 1 == 2 * STEPS - 1:
+                hold_own_part((k - 1) // STEPS)
+            if 10 <= slot < 10 + Q:
+                shared_gate(slot - 10)
+            if slot == 20:
+                load_shared_part(0)
+                load_shared_part(1)
+            if slot == 22:
+                finish(0)
+                load_shared_part(2)
+            if slot == 23:
+                finish(1)
+                load_shared_part(3)
+            if k - 1 == 3 * STEPS - 1 or k - 1 == 4 * STEPS - 1:
+                finish((k - 1) // STEPS)

@@ -21,18 +21,13 @@ PACK = 4
 SHARED = T
 B_TILES = B // P
 
-UNITS = P // E
-STEP_TILES = 4
-STEP_COLS = STEP_TILES * P
+HALF = E // 2
+V_TILES = V // P
+STEP_COLS = HALF * P
 STEPS = V * E // STEP_COLS
 ALL_STEPS = T * STEPS
 CHUNK_COLS = 2 * STEP_COLS
-TILES = V * E // P
-RELU_STEP = STEPS - 1
-BIAS_TILES = RELU_STEP * STEP_TILES
-
-HALF = E // 2
-V_TILES = V // P
+TH = T * B_TILES
 OWN_ENGINES = ("vector", "scalar")
 SHARED_ENGINES = ("scalar", "vector")
 QB = 32
@@ -43,24 +38,28 @@ def tile_plelayer_pb_kernel(tc, task_h, share_h, ews1, ebs1, ew1, eb1, gate_pre1
     nc = tc.nc
     with ExitStack() as stack:
         keep = stack.enter_context(tc.tile_pool(name="keep", bufs=1))
-        raw_pool = stack.enter_context(tc.tile_pool(name="raw", bufs=8))
-        grouped_pool = stack.enter_context(tc.tile_pool(name="grouped", bufs=6))
-        codes_pool = stack.enter_context(tc.tile_pool(name="codes", bufs=6))
+        raw_pool = stack.enter_context(tc.tile_pool(name="raw", bufs=7))
+        grouped_pool = stack.enter_context(tc.tile_pool(name="grouped", bufs=5))
+        codes_pool = stack.enter_context(tc.tile_pool(name="codes", bufs=5))
+        acts_pool = stack.enter_context(tc.tile_pool(name="acts", bufs=3))
         work = stack.enter_context(tc.tile_pool(name="work", bufs=2))
         gated_pool = stack.enter_context(tc.tile_pool(name="gated", bufs=3))
         product_pool = stack.enter_context(tc.psum_pool(name="product", bufs=4))
         turned_pool = stack.enter_context(tc.psum_pool(name="turned", bufs=2))
         sums_pool = stack.enter_context(tc.psum_pool(name="sums", bufs=2))
-        stack.enter_context(tc.manual_schedule())
 
         identity = keep.tile([P, P], F32)
         make_identity(nc, identity[:])
 
-        acts = keep.tile([P, T + 1, B_TILES, U], BF16)
+        acts = {}
 
         def load_acts(m):
             src = share_h if m == SHARED else task_h[m]
-            nc.sync.dma_start(out=acts[:, m], in_=src.rearrange("(h p) u -> p h u", p=P))
+            rows = acts_pool.tile([P, B_TILES * U], BF16, tag="acts", name="act_rows")
+            nc.sync.dma_start(
+                out=rows[:].rearrange("p (h u) -> p h u", h=B_TILES), in_=src.rearrange("(h p) u -> p h u", p=P)
+            )
+            acts[m] = rows
 
         def load_chunk(weights, c):
             raw = raw_pool.tile([P, PACK, CHUNK_COLS], BF16, tag="raw")
@@ -75,8 +74,10 @@ def tile_plelayer_pb_kernel(tc, task_h, share_h, ews1, ebs1, ew1, eb1, gate_pre1
             out=gate_bias[:].rearrange("p t g -> p (t g)"),
             in_=gb1.rearrange("t g -> (t g)").partition_broadcast(P),
         )
-        bias_rows = keep.tile([P, P], BF16)
-        nc.scalar.dma_start(out=bias_rows[:], in_=eb1.rearrange("t (j x) e -> (t j) (x e)", x=UNITS))
+        bias_in = keep.tile([P, T, V_TILES, E], BF16)
+        nc.scalar.dma_start(
+            out=bias_in[:].rearrange("p t c e -> p (t c) e"), in_=eb1.rearrange("t (c p) e -> p (t c) e", p=P)
+        )
         gate_in2 = keep.tile([P, T * Q, G], BF16)
         for r in range(HALF):
             nc.scalar.dma_start(
@@ -96,18 +97,10 @@ def tile_plelayer_pb_kernel(tc, task_h, share_h, ews1, ebs1, ew1, eb1, gate_pre1
         for t in range(1, T):
             load_acts(t)
 
-        select = keep.tile([P, UNITS], F32)
-        nc.vector.tensor_reduce(
-            out=select[:], in_=identity[:].rearrange("p (v e) -> p v e", e=E), axis=AXIS.X, op=ALU.add
-        )
-        bias_f32 = keep.tile([P, P], F32)
-        nc.vector.tensor_copy(out=bias_f32[:], in_=bias_rows[:])
-        bias_bank = turned_pool.tile([P, P], F32, tag="turned")
-        nc.tensor.transpose(out=bias_bank[:], in_=bias_f32[:], identity=identity[:])
-        bias = keep.tile([P, T, TILES], F32)
-        nc.vector.tensor_copy(out=bias[:].rearrange("p t j -> p (t j)"), in_=bias_bank[:])
-        minus_bias = keep.tile([P, T, TILES], F32)
-        nc.vector.tensor_scalar(out=minus_bias[:], in0=bias[:], scalar1=-1.0, scalar2=None, op0=ALU.mult)
+        identity_bf16 = keep.tile([P, P], BF16)
+        nc.vector.tensor_copy(out=identity_bf16[:], in_=identity[:])
+        minus_bias = keep.tile([P, T, V_TILES, E], F32)
+        nc.vector.tensor_scalar(out=minus_bias[:], in0=bias_in[:], scalar1=-1.0, scalar2=None, op0=ALU.mult)
 
         def softmax_numerators(logits_in, blocks, name):
             logits = keep.tile([P, T * blocks, G], F32, name="logits_" + name)
@@ -130,43 +123,64 @@ def tile_plelayer_pb_kernel(tc, task_h, share_h, ews1, ebs1, ew1, eb1, gate_pre1
             nc.vector.reciprocal(out=inverse[:], in_=total[:])
             return powers, inverse
 
-        gate_of_column = keep.tile([P, T, B], F32)
+        own_gates = keep.tile([P, TH, E], F32)
+        spread_gates = keep.tile([P, T, E, B], F32)
+        split_gates = keep.tile([P, TH, 2, E], BF16)
+        gate_rows = keep.tile([P, TH, P], BF16)
+        bias_moving = keep.tile([P, V], BF16)
 
         def make_own_gates():
             powers, inverse = softmax_numerators(gate_in, B_TILES, "own")
-            gates = keep.tile([P, T * B_TILES, E], F32)
             nc.vector.tensor_tensor(
-                out=gates[:],
+                out=own_gates[:],
                 in0=powers[:, :, 0:E],
-                in1=inverse[:].unsqueeze(2).to_broadcast([P, T * B_TILES, E]),
+                in1=inverse[:].unsqueeze(2).to_broadcast([P, TH, E]),
                 op=ALU.mult,
             )
-            spread = keep.tile([P, T * B_TILES, UNITS, E], F32)
-            nc.vector.tensor_copy(
-                out=spread[:], in_=gates[:].unsqueeze(2).to_broadcast([P, T * B_TILES, UNITS, E])
+
+        def spread(t, first, last):
+            for pair in range(first // 2, last // 2):
+                bank = turned_pool.tile([P, 2, B], F32, tag="turned")
+                for s in range(2):
+                    for h in range(B_TILES):
+                        e = 2 * pair + s
+                        nc.tensor.transpose(
+                            out=bank[:, s, h * P : (h + 1) * P],
+                            in_=own_gates[:, t * B_TILES + h, e : e + 1].to_broadcast([P, P]),
+                            identity=identity[:],
+                        )
+                nc.scalar.copy(out=spread_gates[:, t, 2 * pair : 2 * pair + 2], in_=bank[:])
+
+        def make_bias_term():
+            nc.vector.tensor_copy(out=split_gates[:, :, 0], in_=own_gates[:])
+            nc.vector.tensor_tensor(out=split_gates[:, :, 1], in0=own_gates[:], in1=split_gates[:, :, 0], op=ALU.subtract)
+            row_of = keep.tile([P, TH], F32)
+            nc.vector.tensor_reduce(
+                out=row_of[:], in_=identity[:].rearrange("p (x g) -> p x g", g=G), axis=AXIS.X, op=ALU.add
             )
-            for pair in range(T // 2):
-                bank = turned_pool.tile([P, 2 * B], F32, tag="turned")
-                for i in range(2 * B_TILES):
-                    nc.tensor.transpose(
-                        out=bank[:, i * P : (i + 1) * P],
-                        in_=spread[:, pair * 2 * B_TILES + i].rearrange("p v e -> p (v e)"),
-                        identity=identity[:],
-                    )
-                nc.scalar.copy(
-                    out=gate_of_column[:, 2 * pair : 2 * pair + 2].rearrange("p t b -> p (t b)"), in_=bank[:]
+            bank = turned_pool.tile([P, P], BF16, tag="turned", name="gate_bank")
+            nc.tensor.transpose(
+                out=bank[:], in_=split_gates[:].rearrange("p x s e -> p (x s e)"), identity=identity_bf16[:]
+            )
+            nc.vector.tensor_tensor(
+                out=gate_rows[:],
+                in0=bank[:].unsqueeze(1).to_broadcast([P, TH, P]),
+                in1=row_of[:].unsqueeze(2).to_broadcast([P, TH, P]),
+                op=ALU.mult,
+            )
+            bias_spread = keep.tile([P, V_TILES, T, 2 * B_TILES, E], BF16)
+            for c in range(V_TILES):
+                nc.vector.tensor_copy(
+                    out=bias_spread[:, c], in_=bias_in[:, :, c].unsqueeze(2).to_broadcast([P, T, 2 * B_TILES, E])
                 )
-
-        bias_moving = keep.tile([P, T, BIAS_TILES, UNITS], F32)
-
-        def make_bias_moving(first, last, engine):
-            shape = [P, last - first, BIAS_TILES, UNITS]
-            engine.tensor_tensor(
-                out=bias_moving[:, first:last],
-                in0=bias[:, first:last, 0:BIAS_TILES].unsqueeze(3).to_broadcast(shape),
-                in1=select[:].unsqueeze(1).unsqueeze(1).to_broadcast(shape),
-                op=ALU.mult,
-            )
+            bank = turned_pool.tile([P, V], BF16, tag="turned", name="bias_bank")
+            for c in range(V_TILES):
+                nc.tensor.transpose(
+                    out=bank[:, c * P : (c + 1) * P],
+                    in_=bias_spread[:, c].rearrange("p t x e -> p (t x e)"),
+                    identity=identity_bf16[:],
+                )
+            nc.scalar.copy(out=bias_moving[:], in_=bank[:])
 
         block_gates = keep.tile([P, 2, Q, T, QB], F32)
         shared_bias = keep.tile([P, V_TILES, E], F32)
@@ -204,16 +218,13 @@ def tile_plelayer_pb_kernel(tc, task_h, share_h, ews1, ebs1, ew1, eb1, gate_pre1
 
         act_codes = keep.tile([P, T + 1, B], U32, align_bytes=64)
         act_scales = keep.tile([P, T + 1, B], U8, align_bytes=64)
-        act_words = acts[:].rearrange("p m h u -> p (m h u)").bitcast(F32).rearrange(
-            "p (m h j w) -> p m h w j", m=T + 1, h=B_TILES, w=2
-        )
-
         def quantise_activations(m):
+            act_words = acts[m][:].bitcast(F32).rearrange("p (h j w) -> p h w j", h=B_TILES, w=2)
             bank = turned_pool.tile([P, 2, B], F32, tag="turned")
             for h in range(B_TILES):
                 for w in range(2):
                     nc.tensor.transpose(
-                        out=bank[:, w, h * P : (h + 1) * P], in_=act_words[:, m, h, w, :], identity=identity[:]
+                        out=bank[:, w, h * P : (h + 1) * P], in_=act_words[:, h, w, :], identity=identity[:]
                     )
             side_by_side = work.tile([P, B * PACK], BF16, align_bytes=64)
             nc.vector.tensor_copy(
@@ -241,7 +252,7 @@ def tile_plelayer_pb_kernel(tc, task_h, share_h, ews1, ebs1, ew1, eb1, gate_pre1
         def multiply(weights, m):
             codes, scales = weights
             banks = []
-            for first in range(0, STEP_TILES, 2):
+            for first in range(0, HALF, 2):
                 bank = product_pool.tile([P, 2, B], F32, tag="product")
                 for s in range(2):
                     cols = slice((first + s) * P, (first + s + 1) * P)
@@ -257,92 +268,65 @@ def tile_plelayer_pb_kernel(tc, task_h, share_h, ews1, ebs1, ew1, eb1, gate_pre1
                 banks.append(bank)
             return banks
 
+        def regroup(raw, s, engine):
+            grouped = grouped_pool.tile([P, HALF, P, PACK], BF16, tag="grouped", align_bytes=64)
+            src = raw[:].rearrange("p f (v e) -> p f v e", e=E)[:, :, :, s * HALF : (s + 1) * HALF]
+            copy(grouped[:].rearrange("p e v f -> p v f e"), src.rearrange("p f v e -> p v f e"), engine)
+            return grouped
+
         own_grouped, own_weights, own_banks, own_gated = {}, {}, {}, {}
 
         def own_copy_in(k):
-            grouped = grouped_pool.tile([P, STEP_COLS, PACK], BF16, tag="grouped", align_bytes=64)
-            cols = slice((k % 2) * STEP_COLS, (k % 2 + 1) * STEP_COLS)
-            copy(grouped[:], own_raw[k // 2][:, :, cols].rearrange("p f c -> p c f"), OWN_ENGINES[k % len(OWN_ENGINES)])
-            own_grouped[k] = grouped
+            own_grouped[k] = regroup(own_raw[k // 2], k % 2, OWN_ENGINES[k % len(OWN_ENGINES)])
 
         def own_quantise(k):
-            own_weights[k] = quantise(own_grouped[k][:].rearrange("p c f -> p (c f)"))
+            own_weights[k] = quantise(own_grouped[k][:].rearrange("p e v f -> p (e v f)"))
 
         def own_multiply(k):
             own_banks[k] = multiply(own_weights[k], k // STEPS)
 
         def own_gate(k):
-            t, step = k // STEPS, k % STEPS
-            gated = gated_pool.tile([P, STEP_TILES, B], F32, tag="gated")
-            if step == RELU_STEP:
-                relu = work.tile([P, STEP_TILES, B], F32, tag="relu")
-                for i in range(STEP_TILES):
-                    j = step * STEP_TILES + i
-                    nc.scalar.activation(
-                        out=relu[:, i, :],
-                        in_=own_banks[k][i // 2][:, i % 2, :],
-                        func=ACT.Relu,
-                        bias=bias[:, t, j : j + 1],
-                        scale=1.0,
-                    )
-                nc.vector.tensor_tensor(
-                    out=gated[:],
-                    in0=relu[:],
-                    in1=gate_of_column[:, t, :].unsqueeze(1).to_broadcast([P, STEP_TILES, B]),
-                    op=ALU.mult,
+            t, vt, s = k // STEPS, k % STEPS // 2, k % 2
+            gated = gated_pool.tile([P, HALF, B], F32, tag="gated")
+            for i in range(HALF):
+                e = s * HALF + i
+                nc.vector.scalar_tensor_tensor(
+                    out=gated[:, i, :],
+                    in0=own_banks[k][i // 2][:, i % 2, :],
+                    scalar=minus_bias[:, t, vt, e : e + 1],
+                    in1=spread_gates[:, t, e, :],
+                    op0=ALU.max,
+                    op1=ALU.mult,
                 )
-            else:
-                for i in range(STEP_TILES):
-                    j = step * STEP_TILES + i
-                    nc.vector.scalar_tensor_tensor(
-                        out=gated[:, i, :],
-                        in0=own_banks[k][i // 2][:, i % 2, :],
-                        scalar=minus_bias[:, t, j : j + 1],
-                        in1=gate_of_column[:, t, :],
-                        op0=ALU.max,
-                        op1=ALU.mult,
-                    )
             own_gated[k] = gated
 
         sums = {}
 
         def own_add(k):
-            t, step = k // STEPS, k % STEPS
-            if step == 0:
+            t, vt, s = k // STEPS, k % STEPS // 2, k % 2
+            if k % STEPS == 0:
                 for h in range(B_TILES):
                     bank = sums_pool.tile([P, V], F32, tag="sums", name="sum_bank")
                     nc.tensor.matmul(
-                        out=bank[:, 0 : BIAS_TILES * UNITS],
-                        lhsT=gate_of_column[:, t, h * P : (h + 1) * P],
-                        rhs=bias_moving[:, t].rearrange("p j v -> p (j v)"),
-                        start=True,
-                        stop=False,
+                        out=bank[:], lhsT=gate_rows[:, t * B_TILES + h, :], rhs=bias_moving[:], start=True, stop=False
                     )
                     sums[t, h] = bank
-            for i in range(STEP_TILES):
-                j = step * STEP_TILES + i
+            for i in range(HALF):
                 for h in range(B_TILES):
                     nc.tensor.matmul(
-                        out=sums[t, h][:, j * UNITS : (j + 1) * UNITS],
+                        out=sums[t, h][:, vt * P : (vt + 1) * P],
                         lhsT=own_gated[k][:, i, h * P : (h + 1) * P],
-                        rhs=select[:],
+                        rhs=identity[:],
+                        is_transpose=True,
                         start=False,
-                        stop=(j == TILES - 1),
+                        stop=(k % STEPS == STEPS - 1 and i == HALF - 1),
                     )
 
         shared_grouped, shared_hidden = {}, {}
         hidden_by_sample = keep.tile([P, 2, Q, V], F32)
 
         def shared_copy_in(i):
-            vt, s = i // 2, i % 2
-            grouped = grouped_pool.tile([P, HALF, P, PACK], BF16, tag="grouped", align_bytes=64)
-            src = shared_raw[vt][:].rearrange("p f (v e) -> p f v e", e=E)[:, :, :, s * HALF : (s + 1) * HALF]
-            copy(
-                grouped[:].rearrange("p e v f -> p v f e"),
-                src.rearrange("p f v e -> p v f e"),
-                SHARED_ENGINES[i % len(SHARED_ENGINES)],
-            )
-            shared_grouped[i] = grouped
+            shared_grouped[i] = regroup(shared_raw[i // 2], i % 2, SHARED_ENGINES[i % len(SHARED_ENGINES)])
 
         def shared_multiply(i):
             vt, s = i // 2, i % 2
@@ -392,7 +376,7 @@ def tile_plelayer_pb_kernel(tc, task_h, share_h, ews1, ebs1, ew1, eb1, gate_pre1
             nc.scalar.copy(out=shared_sum[q // 2][:, q % 2, :], in_=bank[:])
             if q % 2 == 1:
                 for t in range(T):
-                    nc.sync.dma_start(
+                    nc.scalar.dma_start(
                         out=out[t].rearrange("(q b) v -> b q v", b=QB)[:, q - 1 : q + 1, :],
                         in_=shared_sum[q // 2][t * QB : (t + 1) * QB],
                     )
@@ -413,7 +397,7 @@ def tile_plelayer_pb_kernel(tc, task_h, share_h, ews1, ebs1, ew1, eb1, gate_pre1
             own_part[t] = own
 
         def finish(t):
-            result = work.tile([P, B_TILES, V], F32, tag="relu", name="result")
+            result = work.tile([P, B_TILES, V], F32, tag="result", name="result")
             if t in own_part:
                 nc.gpsimd.tensor_tensor(out=result[:], in0=own_part[t][:], in1=shared_part[t][:], op=ALU.add)
             else:
@@ -433,11 +417,11 @@ def tile_plelayer_pb_kernel(tc, task_h, share_h, ews1, ebs1, ew1, eb1, gate_pre1
                 shared_copy_in(slot + 1)
             if slot == -LEAD:
                 make_own_gates()
-                make_bias_moving(0, 1, nc.vector)
+                spread(0, 0, E)
+                make_bias_term()
                 quantise_activations(SHARED)
             if slot == -1:
                 make_shared_gates()
-                make_bias_moving(1, T, nc.gpsimd)
             if 0 <= k + 2 < ALL_STEPS:
                 own_quantise(k + 2)
             if 0 <= k + 1 < ALL_STEPS:
@@ -456,6 +440,9 @@ def tile_plelayer_pb_kernel(tc, task_h, share_h, ews1, ebs1, ew1, eb1, gate_pre1
                     own_raw[c] = load_chunk(ew1[c // V_TILES], c % V_TILES)
             if slot in (2, 4, 6):
                 quantise_activations(slot // 2)
+            if slot % STEPS in (3, 4, 5, 6) and slot < (T - 1) * STEPS:
+                first = (slot % STEPS - 3) * 2
+                spread(slot // STEPS + 1, first, first + 2)
             if k - 1 == STEPS - 1 or k - 1 == 2 * STEPS - 1:
                 hold_own_part((k - 1) // STEPS)
             if 10 <= slot < 10 + Q:

@@ -123,7 +123,8 @@ def tile_plelayer_pb_kernel(tc, task_h, share_h, ews1, ebs1, ew1, eb1, gate_pre1
             nc.vector.reciprocal(out=inverse[:], in_=total[:])
             return powers, inverse
 
-        own_gates = keep.tile([P, TH, E], F32)
+        own_gates = keep.tile([P, TH, G], F32)
+        gate_columns = keep.tile([P, P], F32)
         spread_gates = keep.tile([P, T, E, B], F32)
         split_gates = keep.tile([P, TH, 2, E], BF16)
         gate_rows = keep.tile([P, TH, P], BF16)
@@ -133,10 +134,26 @@ def tile_plelayer_pb_kernel(tc, task_h, share_h, ews1, ebs1, ew1, eb1, gate_pre1
             powers, inverse = softmax_numerators(gate_in, B_TILES, "own")
             nc.vector.tensor_tensor(
                 out=own_gates[:],
-                in0=powers[:, :, 0:E],
-                in1=inverse[:].unsqueeze(2).to_broadcast([P, TH, E]),
+                in0=powers[:],
+                in1=inverse[:].unsqueeze(2).to_broadcast([P, TH, G]),
                 op=ALU.mult,
             )
+
+        def park_gates():
+            bank = turned_pool.tile([P, P], F32, tag="turned", name="gates_bank")
+            nc.tensor.transpose(
+                out=bank[:], in_=own_gates[:].rearrange("p x g -> p (x g)"), identity=identity[:]
+            )
+            nc.scalar.copy(out=gate_columns[:], in_=bank[:])
+            park = out[T - 1, 0 : P * P // V].rearrange("r (s b) -> (r s) b", b=P)
+            nc.scalar.dma_start(out=park, in_=gate_columns[:])
+            for t in range(1, T):
+                for h in range(B_TILES):
+                    first = (t * B_TILES + h) * G
+                    nc.sync.dma_start(
+                        out=spread_gates[:, t, :, h * P : (h + 1) * P],
+                        in_=park[first : first + E].partition_broadcast(P),
+                    )
 
         def spread(t, first, last):
             for pair in range(first // 2, last // 2):
@@ -152,8 +169,10 @@ def tile_plelayer_pb_kernel(tc, task_h, share_h, ews1, ebs1, ew1, eb1, gate_pre1
                 nc.scalar.copy(out=spread_gates[:, t, 2 * pair : 2 * pair + 2], in_=bank[:])
 
         def make_bias_term():
-            nc.vector.tensor_copy(out=split_gates[:, :, 0], in_=own_gates[:])
-            nc.vector.tensor_tensor(out=split_gates[:, :, 1], in0=own_gates[:], in1=split_gates[:, :, 0], op=ALU.subtract)
+            nc.vector.tensor_copy(out=split_gates[:, :, 0], in_=own_gates[:, :, 0:E])
+            nc.vector.tensor_tensor(
+                out=split_gates[:, :, 1], in0=own_gates[:, :, 0:E], in1=split_gates[:, :, 0], op=ALU.subtract
+            )
             row_of = keep.tile([P, TH], F32)
             nc.vector.tensor_reduce(
                 out=row_of[:], in_=identity[:].rearrange("p (x g) -> p x g", g=G), axis=AXIS.X, op=ALU.add
@@ -209,7 +228,7 @@ def tile_plelayer_pb_kernel(tc, task_h, share_h, ews1, ebs1, ew1, eb1, gate_pre1
                 out=mine[:], in0=mine[:], in1=inverse[:].unsqueeze(2).to_broadcast([P, T * Q, 2]), op=ALU.mult
             )
             for s in range(2):
-                nc.vector.tensor_tensor(
+                nc.gpsimd.tensor_tensor(
                     out=block_gates[:, s],
                     in0=mine[:, :, s].rearrange("p (t q) -> p q t", t=T).unsqueeze(3).to_broadcast([P, Q, T, QB]),
                     in1=same_sample[:].unsqueeze(1).unsqueeze(1).to_broadcast([P, Q, T, QB]),
@@ -227,7 +246,7 @@ def tile_plelayer_pb_kernel(tc, task_h, share_h, ews1, ebs1, ew1, eb1, gate_pre1
                         out=bank[:, w, h * P : (h + 1) * P], in_=act_words[:, h, w, :], identity=identity[:]
                     )
             side_by_side = work.tile([P, B * PACK], BF16, align_bytes=64)
-            nc.vector.tensor_copy(
+            nc.scalar.copy(
                 out=side_by_side[:].bitcast(F32).rearrange("p (b w) -> p b w", w=2),
                 in_=bank[:].rearrange("p w b -> p b w"),
             )
@@ -239,7 +258,7 @@ def tile_plelayer_pb_kernel(tc, task_h, share_h, ews1, ebs1, ew1, eb1, gate_pre1
             if engine == "vector":
                 nc.vector.tensor_copy(out=dst, in_=src)
             elif engine == "scalar":
-                nc.scalar.copy(out=dst, in_=src)
+                nc.scalar.copy(out=dst.rearrange("p v f e -> p v e f"), in_=src.rearrange("p v f e -> p v e f"))
             else:
                 nc.gpsimd.tensor_scalar(out=dst, in0=src, scalar1=1.0, scalar2=0.0, op0=ALU.mult, op1=ALU.add)
 
@@ -354,10 +373,7 @@ def tile_plelayer_pb_kernel(tc, task_h, share_h, ews1, ebs1, ew1, eb1, gate_pre1
                         identity=identity[:],
                     )
                 dst = hidden_by_sample[:, s, first : first + 4, vt * P : (vt + 1) * P]
-                if first == 0:
-                    nc.vector.tensor_copy(out=dst, in_=bank[:])
-                else:
-                    nc.scalar.copy(out=dst, in_=bank[:])
+                nc.scalar.copy(out=dst, in_=bank[:])
 
         shared_sum = {}
 
@@ -418,6 +434,7 @@ def tile_plelayer_pb_kernel(tc, task_h, share_h, ews1, ebs1, ew1, eb1, gate_pre1
             if slot == -LEAD:
                 make_own_gates()
                 spread(0, 0, E)
+                park_gates()
                 make_bias_term()
                 quantise_activations(SHARED)
             if slot == -1:
@@ -440,9 +457,6 @@ def tile_plelayer_pb_kernel(tc, task_h, share_h, ews1, ebs1, ew1, eb1, gate_pre1
                     own_raw[c] = load_chunk(ew1[c // V_TILES], c % V_TILES)
             if slot in (2, 4, 6):
                 quantise_activations(slot // 2)
-            if slot % STEPS in (3, 4, 5, 6) and slot < (T - 1) * STEPS:
-                first = (slot % STEPS - 3) * 2
-                spread(slot // STEPS + 1, first, first + 2)
             if k - 1 == STEPS - 1 or k - 1 == 2 * STEPS - 1:
                 hold_own_part((k - 1) // STEPS)
             if 10 <= slot < 10 + Q:

@@ -258,7 +258,7 @@ def tile_plelayer_pb_kernel(tc, task_h, share_h, ews1, ebs1, ew1, eb1, gate_pre1
             if engine == "vector":
                 nc.vector.tensor_copy(out=dst, in_=src)
             elif engine == "scalar":
-                nc.scalar.copy(out=dst.rearrange("p v f e -> p v e f"), in_=src.rearrange("p v f e -> p v e f"))
+                nc.scalar.copy(out=dst, in_=src)
             else:
                 nc.gpsimd.tensor_scalar(out=dst, in0=src, scalar1=1.0, scalar2=0.0, op0=ALU.mult, op1=ALU.add)
 

@@ -29,7 +29,7 @@ ALL_STEPS = T * STEPS
 CHUNK_COLS = 2 * STEP_COLS
 TH = T * B_TILES
 OWN_ENGINES = ("vector", "scalar")
-SHARED_ENGINES = ("scalar", "vector")
+SHARED_ENGINES = ("vector", "vector")
 QB = 32
 Q = B // QB
 
@@ -44,8 +44,8 @@ def tile_plelayer_pb_kernel(tc, task_h, share_h, ews1, ebs1, ew1, eb1, gate_pre1
         acts_pool = stack.enter_context(tc.tile_pool(name="acts", bufs=3))
         work = stack.enter_context(tc.tile_pool(name="work", bufs=2))
         gated_pool = stack.enter_context(tc.tile_pool(name="gated", bufs=3))
-        product_pool = stack.enter_context(tc.psum_pool(name="product", bufs=4))
-        turned_pool = stack.enter_context(tc.psum_pool(name="turned", bufs=2))
+        product_pool = stack.enter_context(tc.psum_pool(name="product", bufs=3))
+        turned_pool = stack.enter_context(tc.psum_pool(name="turned", bufs=3))
         sums_pool = stack.enter_context(tc.psum_pool(name="sums", bufs=2))
 
         identity = keep.tile([P, P], F32)
@@ -78,11 +78,6 @@ def tile_plelayer_pb_kernel(tc, task_h, share_h, ews1, ebs1, ew1, eb1, gate_pre1
         nc.scalar.dma_start(
             out=bias_in[:].rearrange("p t c e -> p (t c) e"), in_=eb1.rearrange("t (c p) e -> p (t c) e", p=P)
         )
-        gate_in2 = keep.tile([P, T * Q, G], BF16)
-        for r in range(HALF):
-            nc.scalar.dma_start(
-                out=gate_in2[r * QB : (r + 1) * QB], in_=gate_pre1.rearrange("t (q b) g -> b (t q) g", b=QB)
-            )
         shared_bias_in = keep.tile([P, V_TILES, E], BF16)
         nc.scalar.dma_start(out=shared_bias_in[:], in_=ebs1.rearrange("(c p) e -> p c e", p=P))
 
@@ -181,12 +176,8 @@ def tile_plelayer_pb_kernel(tc, task_h, share_h, ews1, ebs1, ew1, eb1, gate_pre1
             nc.tensor.transpose(
                 out=bank[:], in_=split_gates[:].rearrange("p x s e -> p (x s e)"), identity=identity_bf16[:]
             )
-            nc.vector.tensor_tensor(
-                out=gate_rows[:],
-                in0=bank[:].unsqueeze(1).to_broadcast([P, TH, P]),
-                in1=row_of[:].unsqueeze(2).to_broadcast([P, TH, P]),
-                op=ALU.mult,
-            )
+            for x in range(TH):
+                nc.scalar.activation(out=gate_rows[:, x, :], in_=bank[:], func=ACT.Copy, scale=row_of[:, x : x + 1])
             bias_spread = keep.tile([P, V_TILES, T, 2 * B_TILES, E], BF16)
             for c in range(V_TILES):
                 nc.vector.tensor_copy(
@@ -214,26 +205,37 @@ def tile_plelayer_pb_kernel(tc, task_h, share_h, ews1, ebs1, ew1, eb1, gate_pre1
             nc.vector.tensor_reduce(
                 out=own_copy[:], in_=identity[:].rearrange("p (r b) -> p r b", b=QB), axis=AXIS.X, op=ALU.add
             )
-            powers, inverse = softmax_numerators(gate_in2, Q, "shared")
-            picked = keep.tile([P, T * Q, 2, HALF], F32)
+            repeated = keep.tile([P, HALF, HALF, QB], F32)
+            nc.gpsimd.tensor_copy(
+                out=repeated[:],
+                in_=gate_columns[:].rearrange("p (q b) -> p q b", b=QB).unsqueeze(2).to_broadcast([P, HALF, HALF, QB]),
+            )
+            bank = turned_pool.tile([P, HALF, TH, G], F32, tag="turned", name="repeated_bank")
+            for q in range(HALF):
+                nc.tensor.transpose(
+                    out=bank[:, q].rearrange("p x g -> p (x g)"),
+                    in_=repeated[:, q].rearrange("p r b -> p (r b)"),
+                    identity=identity[:],
+                )
+            picked = keep.tile([P, HALF * TH, 2, HALF], F32)
             nc.vector.tensor_tensor(
                 out=picked[:],
-                in0=powers[:, :, E:G].rearrange("p x (s e) -> p x s e", e=HALF),
-                in1=own_copy[:].unsqueeze(1).unsqueeze(1).to_broadcast([P, T * Q, 2, HALF]),
+                in0=bank[:, :, :, E:G].rearrange("p q x (s e) -> p (q x) s e", e=HALF),
+                in1=own_copy[:].unsqueeze(1).unsqueeze(1).to_broadcast([P, HALF * TH, 2, HALF]),
                 op=ALU.mult,
             )
-            mine = keep.tile([P, T * Q, 2], F32)
-            nc.vector.tensor_reduce(out=mine[:], in_=picked[:], axis=AXIS.X, op=ALU.add)
-            nc.vector.tensor_tensor(
-                out=mine[:], in0=mine[:], in1=inverse[:].unsqueeze(2).to_broadcast([P, T * Q, 2]), op=ALU.mult
+            mine = keep.tile([P, HALF, T, B_TILES, 2], F32)
+            nc.vector.tensor_reduce(
+                out=mine[:].rearrange("p q t h s -> p (q t h) s"), in_=picked[:], axis=AXIS.X, op=ALU.add
             )
             for s in range(2):
-                nc.gpsimd.tensor_tensor(
-                    out=block_gates[:, s],
-                    in0=mine[:, :, s].rearrange("p (t q) -> p q t", t=T).unsqueeze(3).to_broadcast([P, Q, T, QB]),
-                    in1=same_sample[:].unsqueeze(1).unsqueeze(1).to_broadcast([P, Q, T, QB]),
-                    op=ALU.mult,
-                )
+                for h in range(B_TILES):
+                    nc.vector.tensor_tensor(
+                        out=block_gates[:, s, h * HALF : (h + 1) * HALF],
+                        in0=mine[:, :, :, h, s].unsqueeze(3).to_broadcast([P, HALF, T, QB]),
+                        in1=same_sample[:].unsqueeze(1).unsqueeze(1).to_broadcast([P, HALF, T, QB]),
+                        op=ALU.mult,
+                    )
 
         act_codes = keep.tile([P, T + 1, B], U32, align_bytes=64)
         act_scales = keep.tile([P, T + 1, B], U8, align_bytes=64)

@@ -50,6 +50,8 @@ def tile_plelayer_pb_kernel(tc, task_h, share_h, ews1, ebs1, ew1, eb1, gate_pre1
 
         identity = keep.tile([P, P], F32)
         make_identity(nc, identity[:])
+        warm = keep.tile([P, 1], F32)
+        nc.scalar.activation(out=warm[:], in_=identity[:, 0:1], func=ACT.Exp)
 
         acts = {}
 
@@ -61,16 +63,22 @@ def tile_plelayer_pb_kernel(tc, task_h, share_h, ews1, ebs1, ew1, eb1, gate_pre1
             )
             acts[m] = rows
 
-        def load_chunk(weights, c):
+        def load_chunk(weights, c, parts=1):
             raw = raw_pool.tile([P, PACK, CHUNK_COLS], BF16, tag="raw")
             rows = weights.rearrange("(p f) v e -> p f (v e)", f=PACK)
-            nc.sync.dma_start(out=raw[:], in_=rows[:, :, c * CHUNK_COLS : (c + 1) * CHUNK_COLS])
+            width = CHUNK_COLS // parts
+            for part in range(parts):
+                first = part * width
+                nc.sync.dma_start(
+                    out=raw[:, :, first : first + width],
+                    in_=rows[:, :, c * CHUNK_COLS + first : c * CHUNK_COLS + first + width],
+                )
             return raw
 
         gate_in = keep.tile([P, T * B_TILES, G], BF16)
-        nc.scalar.dma_start(out=gate_in[:], in_=gate_pre1.rearrange("t (h p) g -> p (t h) g", p=P))
+        nc.sync.dma_start(out=gate_in[:], in_=gate_pre1.rearrange("t (h p) g -> p (t h) g", p=P))
         gate_bias = keep.tile([P, T, G], BF16)
-        nc.scalar.dma_start(
+        nc.sync.dma_start(
             out=gate_bias[:].rearrange("p t g -> p (t g)"),
             in_=gb1.rearrange("t g -> (t g)").partition_broadcast(P),
         )
@@ -83,7 +91,7 @@ def tile_plelayer_pb_kernel(tc, task_h, share_h, ews1, ebs1, ew1, eb1, gate_pre1
 
         load_acts(0)
         own_raw, shared_raw = {}, {}
-        own_raw[0] = load_chunk(ew1[0], 0)
+        own_raw[0] = load_chunk(ew1[0], 0, 2)
         load_acts(SHARED)
         shared_raw[0] = load_chunk(ews1, 0)
         for c in range(1, V_TILES):
@@ -258,7 +266,7 @@ def tile_plelayer_pb_kernel(tc, task_h, share_h, ews1, ebs1, ew1, eb1, gate_pre1
 
         def copy(dst, src, engine):
             if engine == "vector":
-                nc.vector.tensor_copy(out=dst, in_=src)
+                nc.vector.tensor_copy(out=dst.rearrange("p v f e -> p v e f"), in_=src.rearrange("p v f e -> p v e f"))
             elif engine == "scalar":
                 nc.scalar.copy(out=dst, in_=src)
             else:
@@ -289,16 +297,22 @@ def tile_plelayer_pb_kernel(tc, task_h, share_h, ews1, ebs1, ew1, eb1, gate_pre1
                 banks.append(bank)
             return banks
 
-        def regroup(raw, s, engine):
+        def regroup(raw, s, engine, parts=1):
             grouped = grouped_pool.tile([P, HALF, P, PACK], BF16, tag="grouped", align_bytes=64)
             src = raw[:].rearrange("p f (v e) -> p f v e", e=E)[:, :, :, s * HALF : (s + 1) * HALF]
-            copy(grouped[:].rearrange("p e v f -> p v f e"), src.rearrange("p f v e -> p v f e"), engine)
+            for part in range(parts):
+                units = slice(part * P // parts, (part + 1) * P // parts)
+                copy(
+                    grouped[:, :, units].rearrange("p e v f -> p v f e"),
+                    src[:, :, units].rearrange("p f v e -> p v f e"),
+                    engine,
+                )
             return grouped
 
         own_grouped, own_weights, own_banks, own_gated = {}, {}, {}, {}
 
         def own_copy_in(k):
-            own_grouped[k] = regroup(own_raw[k // 2], k % 2, OWN_ENGINES[k % len(OWN_ENGINES)])
+            own_grouped[k] = regroup(own_raw[k // 2], k % 2, OWN_ENGINES[k % len(OWN_ENGINES)], 2 if k < 2 else 1)
 
         def own_quantise(k):
             own_weights[k] = quantise(own_grouped[k][:].rearrange("p e v f -> p (e v f)"))
@@ -427,6 +441,8 @@ def tile_plelayer_pb_kernel(tc, task_h, share_h, ews1, ebs1, ew1, eb1, gate_pre1
 
         LEAD = 3
         quantise_activations(0)
+        make_own_gates()
+        spread(0, 0, E)
         for slot in range(-LEAD, ALL_STEPS + 1):
             k = slot
             if 0 <= k + LEAD < ALL_STEPS:
@@ -434,8 +450,6 @@ def tile_plelayer_pb_kernel(tc, task_h, share_h, ews1, ebs1, ew1, eb1, gate_pre1
             if 0 <= slot + 1 < 2 * V_TILES:
                 shared_copy_in(slot + 1)
             if slot == -LEAD:
-                make_own_gates()
-                spread(0, 0, E)
                 park_gates()
                 make_bias_term()
                 quantise_activations(SHARED)

@@ -266,7 +266,7 @@ def tile_plelayer_pb_kernel(tc, task_h, share_h, ews1, ebs1, ew1, eb1, gate_pre1
 
         def copy(dst, src, engine):
             if engine == "vector":
-                nc.vector.tensor_copy(out=dst.rearrange("p v f e -> p v e f"), in_=src.rearrange("p v f e -> p v e f"))
+                nc.vector.tensor_copy(out=dst, in_=src)
             elif engine == "scalar":
                 nc.scalar.copy(out=dst, in_=src)
             else:
@@ -303,8 +303,8 @@ def tile_plelayer_pb_kernel(tc, task_h, share_h, ews1, ebs1, ew1, eb1, gate_pre1
             for part in range(parts):
                 units = slice(part * P // parts, (part + 1) * P // parts)
                 copy(
-                    grouped[:, :, units].rearrange("p e v f -> p v f e"),
-                    src[:, :, units].rearrange("p f v e -> p v f e"),
+                    grouped[:, :, units].rearrange("p e (v w) f -> p v f w e", w=2),
+                    src[:, :, units].rearrange("p f (v w) e -> p v f w e", w=2),
                     engine,
                 )
             return grouped

@@ -303,8 +303,8 @@ def tile_plelayer_pb_kernel(tc, task_h, share_h, ews1, ebs1, ew1, eb1, gate_pre1
             for part in range(parts):
                 units = slice(part * P // parts, (part + 1) * P // parts)
                 copy(
-                    grouped[:, :, units].rearrange("p e (v w) f -> p v f w e", w=2),
-                    src[:, :, units].rearrange("p f (v w) e -> p v f w e", w=2),
+                    grouped[:, :, units].rearrange("p e v f -> p v f e"),
+                    src[:, :, units].rearrange("p f v e -> p v f e"),
                     engine,
                 )
             return grouped
@@ -337,24 +337,45 @@ def tile_plelayer_pb_kernel(tc, task_h, share_h, ews1, ebs1, ew1, eb1, gate_pre1
 
         sums = {}
 
+        def add_bias_term(t, h, out_columns, first, start):
+            nc.tensor.matmul(
+                out=out_columns,
+                lhsT=gate_rows[:, t * B_TILES + h, :],
+                rhs=bias_moving[:, first : first + out_columns.shape[1]],
+                start=start,
+                stop=False,
+            )
+
+        def sum_columns(t, h, vt):
+            if (t, vt) == (T - 1, V_TILES - 1):
+                return last_bank[0][:, h, :]
+            return sums[t, h][:, vt * P : (vt + 1) * P]
+
+        last_bank = []
+
         def own_add(k):
             t, vt, s = k // STEPS, k % STEPS // 2, k % 2
             if k % STEPS == 0:
                 for h in range(B_TILES):
                     bank = sums_pool.tile([P, V], F32, tag="sums", name="sum_bank")
-                    nc.tensor.matmul(
-                        out=bank[:], lhsT=gate_rows[:, t * B_TILES + h, :], rhs=bias_moving[:], start=True, stop=False
-                    )
+                    width = V if t < T - 1 else V - P
+                    add_bias_term(t, h, bank[:, 0:width], 0, True)
                     sums[t, h] = bank
+            if k == ALL_STEPS - 2:
+                bank = turned_pool.tile([P, B_TILES, P], F32, tag="turned", name="last_bank")
+                for h in range(B_TILES):
+                    add_bias_term(t, h, bank[:, h, :], V - P, h == 0)
+                last_bank.append(bank)
+            closes = k % STEPS == STEPS - 1 or k == ALL_STEPS - 3
             for i in range(HALF):
                 for h in range(B_TILES):
                     nc.tensor.matmul(
-                        out=sums[t, h][:, vt * P : (vt + 1) * P],
+                        out=sum_columns(t, h, vt),
                         lhsT=own_gated[k][:, i, h * P : (h + 1) * P],
                         rhs=identity[:],
                         is_transpose=True,
                         start=False,
-                        stop=(k % STEPS == STEPS - 1 and i == HALF - 1),
+                        stop=(closes and i == HALF - 1 and (k < ALL_STEPS - 1 or h == B_TILES - 1)),
                     )
 
         shared_grouped, shared_hidden = {}, {}
@@ -428,10 +449,35 @@ def tile_plelayer_pb_kernel(tc, task_h, share_h, ews1, ebs1, ew1, eb1, gate_pre1
                 nc.scalar.copy(out=own[:, h, :], in_=sums[t, h][:])
             own_part[t] = own
 
+        def finish_last(vt_first, vt_last):
+            t = T - 1
+            cols = slice(vt_first * P, vt_last * P)
+            result = work.tile([P, B_TILES, V], F32, tag="result", name="result")
+            if vt_last == V_TILES:
+                nc.vector.tensor_tensor(
+                    out=result[:, :, cols], in0=last_bank[0][:], in1=shared_part[t][:, :, cols], op=ALU.add
+                )
+            else:
+                for h in range(B_TILES):
+                    nc.vector.tensor_tensor(
+                        out=result[:, h, cols], in0=sums[t, h][:, cols], in1=shared_part[t][:, h, cols], op=ALU.add
+                    )
+            nc.sync.dma_start(
+                out=out[t].rearrange("(h p) v -> p h v", p=P)[:, :, cols], in_=result[:, :, cols]
+            )
+
         def finish(t):
             result = work.tile([P, B_TILES, V], F32, tag="result", name="result")
             if t in own_part:
-                nc.gpsimd.tensor_tensor(out=result[:], in0=own_part[t][:], in1=shared_part[t][:], op=ALU.add)
+                for h in range(B_TILES):
+                    for half in range(2):
+                        cols = slice(half * V // 2, (half + 1) * V // 2)
+                        nc.gpsimd.tensor_tensor(
+                            out=result[:, h, cols],
+                            in0=own_part[t][:, h, cols],
+                            in1=shared_part[t][:, h, cols],
+                            op=ALU.add,
+                        )
             else:
                 for h in range(B_TILES):
                     nc.vector.tensor_tensor(
@@ -486,5 +532,9 @@ def tile_plelayer_pb_kernel(tc, task_h, share_h, ews1, ebs1, ew1, eb1, gate_pre1
             if slot == 23:
                 finish(1)
                 load_shared_part(3)
-            if k - 1 == 3 * STEPS - 1 or k - 1 == 4 * STEPS - 1:
-                finish((k - 1) // STEPS)
+            if k - 1 == 3 * STEPS - 1:
+                finish(T - 2)
+            if k - 1 == ALL_STEPS - 3:
+                finish_last(0, V_TILES - 1)
+            if k - 1 == ALL_STEPS - 1:
+                finish_last(V_TILES - 1, V_TILES)

@@ -238,12 +238,22 @@ def tile_plelayer_pb_kernel(tc, task_h, share_h, ews1, ebs1, ew1, eb1, gate_pre1
             )
             for s in range(2):
                 for h in range(B_TILES):
-                    nc.vector.tensor_tensor(
-                        out=block_gates[:, s, h * HALF : (h + 1) * HALF],
-                        in0=mine[:, :, :, h, s].unsqueeze(3).to_broadcast([P, HALF, T, QB]),
-                        in1=same_sample[:].unsqueeze(1).unsqueeze(1).to_broadcast([P, HALF, T, QB]),
-                        op=ALU.mult,
-                    )
+                    if True:
+                        for q in range(HALF):
+                            for t in range(T):
+                                nc.scalar.activation(
+                                    out=block_gates[:, s, h * HALF + q, t, :],
+                                    in_=same_sample[:],
+                                    func=ACT.Copy,
+                                    scale=mine[:, q, t, h, s : s + 1],
+                                )
+                    else:
+                        nc.vector.tensor_tensor(
+                            out=block_gates[:, s, h * HALF : (h + 1) * HALF],
+                            in0=mine[:, :, :, h, s].unsqueeze(3).to_broadcast([P, HALF, T, QB]),
+                            in1=same_sample[:].unsqueeze(1).unsqueeze(1).to_broadcast([P, HALF, T, QB]),
+                            op=ALU.mult,
+                        )
 
         act_codes = keep.tile([P, T + 1, B], U32, align_bytes=64)
         act_scales = keep.tile([P, T + 1, B], U8, align_bytes=64)
@@ -519,7 +529,7 @@ def tile_plelayer_pb_kernel(tc, task_h, share_h, ews1, ebs1, ew1, eb1, gate_pre1
                     own_raw[c] = load_chunk(ew1[c // V_TILES], c % V_TILES)
             if slot in (2, 4, 6):
                 quantise_activations(slot // 2)
-            if k - 1 == STEPS - 1 or k - 1 == 2 * STEPS - 1:
+            if k - 1 in (STEPS - 1, 2 * STEPS - 1, 3 * STEPS - 1):
                 hold_own_part((k - 1) // STEPS)
             if 10 <= slot < 10 + Q:
                 shared_gate(slot - 10)
@@ -532,7 +542,7 @@ def tile_plelayer_pb_kernel(tc, task_h, share_h, ews1, ebs1, ew1, eb1, gate_pre1
             if slot == 23:
                 finish(1)
                 load_shared_part(3)
-            if k - 1 == 3 * STEPS - 1:
+            if k - 1 == 3 * STEPS + 1:
                 finish(T - 2)
             if k - 1 == ALL_STEPS - 3:
                 finish_last(0, V_TILES - 1)

from contextlib import ExitStack

import concourse.mybir as mybir
from concourse.masks import make_identity

F32 = mybir.dt.float32
BF16 = mybir.dt.bfloat16
U32 = mybir.dt.uint32
U8 = mybir.dt.uint8
FP8X4 = mybir.dt.float8_e4m3fn_x4
ALU = mybir.AluOpType
ACT = mybir.ActivationFunctionType
AXIS = mybir.AxisListType

T, B, U, V, E = 4, 256, 512, 512, 8
G = 2 * E
FLOPS = 2 * (T + 1) * B * U * V * E

P = 128
PACK = 4
SHARED = T
B_TILES = B // P

HALF = E // 2
V_TILES = V // P
STEP_COLS = HALF * P
STEPS = V * E // STEP_COLS
ALL_STEPS = T * STEPS
CHUNK_COLS = 2 * STEP_COLS
TH = T * B_TILES
OWN_ENGINES = ("vector", "scalar")
SHARED_ENGINES = ("vector", "vector")
QB = 32
Q = B // QB


def tile_plelayer_pb_kernel(tc, task_h, share_h, ews1, ebs1, ew1, eb1, gate_pre1, gb1, out):
    nc = tc.nc
    with ExitStack() as stack:
        keep = stack.enter_context(tc.tile_pool(name="keep", bufs=1))
        raw_pool = stack.enter_context(tc.tile_pool(name="raw", bufs=7))
        grouped_pool = stack.enter_context(tc.tile_pool(name="grouped", bufs=5))
        codes_pool = stack.enter_context(tc.tile_pool(name="codes", bufs=5))
        acts_pool = stack.enter_context(tc.tile_pool(name="acts", bufs=3))
        work = stack.enter_context(tc.tile_pool(name="work", bufs=2))
        gated_pool = stack.enter_context(tc.tile_pool(name="gated", bufs=3))
        product_pool = stack.enter_context(tc.psum_pool(name="product", bufs=3))
        turned_pool = stack.enter_context(tc.psum_pool(name="turned", bufs=3))
        sums_pool = stack.enter_context(tc.psum_pool(name="sums", bufs=2))

        identity = keep.tile([P, P], F32)
        make_identity(nc, identity[:])
        warm = keep.tile([P, 1], F32)
        nc.scalar.activation(out=warm[:], in_=identity[:, 0:1], func=ACT.Exp)

        acts = {}

        def load_acts(m):
            src = share_h if m == SHARED else task_h[m]
            rows = acts_pool.tile([P, B_TILES * U], BF16, tag="acts", name="act_rows")
            nc.sync.dma_start(
                out=rows[:].rearrange("p (h u) -> p h u", h=B_TILES), in_=src.rearrange("(h p) u -> p h u", p=P)
            )
            acts[m] = rows

        def load_chunk(weights, c, parts=1):
            raw = raw_pool.tile([P, PACK, CHUNK_COLS], BF16, tag="raw")
            rows = weights.rearrange("(p f) v e -> p f (v e)", f=PACK)
            width = CHUNK_COLS // parts
            for part in range(parts):
                first = part * width
                nc.sync.dma_start(
                    out=raw[:, :, first : first + width],
                    in_=rows[:, :, c * CHUNK_COLS + first : c * CHUNK_COLS + first + width],
                )
            return raw

        gate_in = keep.tile([P, T * B_TILES, G], BF16)
        nc.sync.dma_start(out=gate_in[:], in_=gate_pre1.rearrange("t (h p) g -> p (t h) g", p=P))
        gate_bias = keep.tile([P, T, G], BF16)
        nc.sync.dma_start(
            out=gate_bias[:].rearrange("p t g -> p (t g)"),
            in_=gb1.rearrange("t g -> (t g)").partition_broadcast(P),
        )
        bias_in = keep.tile([P, T, V_TILES, E], BF16)
        nc.scalar.dma_start(
            out=bias_in[:].rearrange("p t c e -> p (t c) e"), in_=eb1.rearrange("t (c p) e -> p (t c) e", p=P)
        )
        shared_bias_in = keep.tile([P, V_TILES, E], BF16)
        nc.scalar.dma_start(out=shared_bias_in[:], in_=ebs1.rearrange("(c p) e -> p c e", p=P))

        load_acts(0)
        own_raw, shared_raw = {}, {}
        own_raw[0] = load_chunk(ew1[0], 0, 2)
        load_acts(SHARED)
        shared_raw[0] = load_chunk(ews1, 0)
        for c in range(1, V_TILES):
            own_raw[c] = load_chunk(ew1[0], c)
            shared_raw[c] = load_chunk(ews1, c)
        for t in range(1, T):
            load_acts(t)

        identity_bf16 = keep.tile([P, P], BF16)
        nc.vector.tensor_copy(out=identity_bf16[:], in_=identity[:])
        minus_bias = keep.tile([P, T, V_TILES, E], F32)
        nc.vector.tensor_scalar(out=minus_bias[:], in0=bias_in[:], scalar1=-1.0, scalar2=None, op0=ALU.mult)

        def softmax_numerators(logits_in, blocks, name):
            logits = keep.tile([P, T * blocks, G], F32, name="logits_" + name)
            nc.vector.tensor_tensor(
                out=logits[:].rearrange("p (t q) g -> p t q g", t=T),
                in0=logits_in[:].rearrange("p (t q) g -> p t q g", t=T),
                in1=gate_bias[:].unsqueeze(2).to_broadcast([P, T, blocks, G]),
                op=ALU.add,
            )
            top = keep.tile([P, T * blocks], F32, name="top_" + name)
            nc.vector.tensor_reduce(out=top[:], in_=logits[:], axis=AXIS.X, op=ALU.max)
            nc.vector.tensor_tensor(
                out=logits[:], in0=logits[:], in1=top[:].unsqueeze(2).to_broadcast([P, T * blocks, G]), op=ALU.subtract
            )
            powers = keep.tile([P, T * blocks, G], F32, name="powers_" + name)
            nc.scalar.activation(out=powers[:], in_=logits[:], func=ACT.Exp)
            total = keep.tile([P, T * blocks], F32, name="total_" + name)
            nc.vector.tensor_reduce(out=total[:], in_=powers[:], axis=AXIS.X, op=ALU.add)
            inverse = keep.tile([P, T * blocks], F32, name="inverse_" + name)
            nc.vector.reciprocal(out=inverse[:], in_=total[:])
            return powers, inverse

        own_gates = keep.tile([P, TH, G], F32)
        gate_columns = keep.tile([P, P], F32)
        spread_gates = keep.tile([P, T, E, B], F32)
        split_gates = keep.tile([P, TH, 2, E], BF16)
        gate_rows = keep.tile([P, TH, P], BF16)
        bias_moving = keep.tile([P, V], BF16)

        def make_own_gates():
            powers, inverse = softmax_numerators(gate_in, B_TILES, "own")
            nc.vector.tensor_tensor(
                out=own_gates[:],
                in0=powers[:],
                in1=inverse[:].unsqueeze(2).to_broadcast([P, TH, G]),
                op=ALU.mult,
            )

        def park_gates():
            bank = turned_pool.tile([P, P], F32, tag="turned", name="gates_bank")
            nc.tensor.transpose(
                out=bank[:], in_=own_gates[:].rearrange("p x g -> p (x g)"), identity=identity[:]
            )
            nc.scalar.copy(out=gate_columns[:], in_=bank[:])
            park = out[T - 1, 0 : P * P // V].rearrange("r (s b) -> (r s) b", b=P)
            nc.scalar.dma_start(out=park, in_=gate_columns[:])
            for t in range(1, T):
                for h in range(B_TILES):
                    first = (t * B_TILES + h) * G
                    nc.sync.dma_start(
                        out=spread_gates[:, t, :, h * P : (h + 1) * P],
                        in_=park[first : first + E].partition_broadcast(P),
                    )

        def spread(t, first, last):
            for pair in range(first // 2, last // 2):
                bank = turned_pool.tile([P, 2, B], F32, tag="turned")
                for s in range(2):
                    for h in range(B_TILES):
                        e = 2 * pair + s
                        nc.tensor.transpose(
                            out=bank[:, s, h * P : (h + 1) * P],
                            in_=own_gates[:, t * B_TILES + h, e : e + 1].to_broadcast([P, P]),
                            identity=identity[:],
                        )
                nc.scalar.copy(out=spread_gates[:, t, 2 * pair : 2 * pair + 2], in_=bank[:])

        def make_bias_term():
            nc.vector.tensor_copy(out=split_gates[:, :, 0], in_=own_gates[:, :, 0:E])
            nc.vector.tensor_tensor(
                out=split_gates[:, :, 1], in0=own_gates[:, :, 0:E], in1=split_gates[:, :, 0], op=ALU.subtract
            )
            row_of = keep.tile([P, TH], F32)
            nc.vector.tensor_reduce(
                out=row_of[:], in_=identity[:].rearrange("p (x g) -> p x g", g=G), axis=AXIS.X, op=ALU.add
            )
            bank = turned_pool.tile([P, P], BF16, tag="turned", name="gate_bank")
            nc.tensor.transpose(
                out=bank[:], in_=split_gates[:].rearrange("p x s e -> p (x s e)"), identity=identity_bf16[:]
            )
            for x in range(TH):
                nc.scalar.activation(out=gate_rows[:, x, :], in_=bank[:], func=ACT.Copy, scale=row_of[:, x : x + 1])
            bias_spread = keep.tile([P, V_TILES, T, 2 * B_TILES, E], BF16)
            for c in range(V_TILES):
                nc.vector.tensor_copy(
                    out=bias_spread[:, c], in_=bias_in[:, :, c].unsqueeze(2).to_broadcast([P, T, 2 * B_TILES, E])
                )
            bank = turned_pool.tile([P, V], BF16, tag="turned", name="bias_bank")
            for c in range(V_TILES):
                nc.tensor.transpose(
                    out=bank[:, c * P : (c + 1) * P],
                    in_=bias_spread[:, c].rearrange("p t x e -> p (t x e)"),
                    identity=identity_bf16[:],
                )
            nc.scalar.copy(out=bias_moving[:], in_=bank[:])

        block_gates = keep.tile([P, 2, Q, T, QB], F32)
        shared_bias = keep.tile([P, V_TILES, E], F32)

        def make_shared_gates():
            nc.vector.tensor_copy(out=shared_bias[:], in_=shared_bias_in[:])
            same_sample = keep.tile([P, QB], F32)
            nc.vector.tensor_reduce(
                out=same_sample[:], in_=identity[:].rearrange("p (r b) -> p b r", b=QB), axis=AXIS.X, op=ALU.add
            )
            own_copy = keep.tile([P, HALF], F32)
            nc.vector.tensor_reduce(
                out=own_copy[:], in_=identity[:].rearrange("p (r b) -> p r b", b=QB), axis=AXIS.X, op=ALU.add
            )
            repeated = keep.tile([P, HALF, HALF, QB], F32)
            nc.gpsimd.tensor_copy(
                out=repeated[:],
                in_=gate_columns[:].rearrange("p (q b) -> p q b", b=QB).unsqueeze(2).to_broadcast([P, HALF, HALF, QB]),
            )
            bank = turned_pool.tile([P, HALF, TH, G], F32, tag="turned", name="repeated_bank")
            for q in range(HALF):
                nc.tensor.transpose(
                    out=bank[:, q].rearrange("p x g -> p (x g)"),
                    in_=repeated[:, q].rearrange("p r b -> p (r b)"),
                    identity=identity[:],
                )
            picked = keep.tile([P, HALF * TH, 2, HALF], F32)
            nc.vector.tensor_tensor(
                out=picked[:],
                in0=bank[:, :, :, E:G].rearrange("p q x (s e) -> p (q x) s e", e=HALF),
                in1=own_copy[:].unsqueeze(1).unsqueeze(1).to_broadcast([P, HALF * TH, 2, HALF]),
                op=ALU.mult,
            )
            mine = keep.tile([P, HALF, T, B_TILES, 2], F32)
            nc.vector.tensor_reduce(
                out=mine[:].rearrange("p q t h s -> p (q t h) s"), in_=picked[:], axis=AXIS.X, op=ALU.add
            )
            for s in range(2):
                for h in range(B_TILES):
                    if True:
                        for q in range(HALF):
                            for t in range(T):
                                nc.scalar.activation(
                                    out=block_gates[:, s, h * HALF + q, t, :],
                                    in_=same_sample[:],
                                    func=ACT.Copy,
                                    scale=mine[:, q, t, h, s : s + 1],
                                )
                    else:
                        nc.vector.tensor_tensor(
                            out=block_gates[:, s, h * HALF : (h + 1) * HALF],
                            in0=mine[:, :, :, h, s].unsqueeze(3).to_broadcast([P, HALF, T, QB]),
                            in1=same_sample[:].unsqueeze(1).unsqueeze(1).to_broadcast([P, HALF, T, QB]),
                            op=ALU.mult,
                        )

        act_codes = keep.tile([P, T + 1, B], U32, align_bytes=64)
        act_scales = keep.tile([P, T + 1, B], U8, align_bytes=64)
        def quantise_activations(m):
            act_words = acts[m][:].bitcast(F32).rearrange("p (h j w) -> p h w j", h=B_TILES, w=2)
            bank = turned_pool.tile([P, 2, B], F32, tag="turned")
            for h in range(B_TILES):
                for w in range(2):
                    nc.tensor.transpose(
                        out=bank[:, w, h * P : (h + 1) * P], in_=act_words[:, h, w, :], identity=identity[:]
                    )
            side_by_side = work.tile([P, B * PACK], BF16, align_bytes=64)
            nc.scalar.copy(
                out=side_by_side[:].bitcast(F32).rearrange("p (b w) -> p b w", w=2),
                in_=bank[:].rearrange("p w b -> p b w"),
            )
            nc.vector.quantize_mx(
                out=act_codes[:, m, :].bitcast(FP8X4), scales=act_scales[:, m, :], in_=side_by_side[:]
            )

        def copy(dst, src, engine):
            if engine == "vector":
                nc.vector.tensor_copy(out=dst, in_=src)
            elif engine == "scalar":
                nc.scalar.copy(out=dst, in_=src)
            else:
                nc.gpsimd.tensor_scalar(out=dst, in0=src, scalar1=1.0, scalar2=0.0, op0=ALU.mult, op1=ALU.add)

        def quantise(grouped):
            codes = codes_pool.tile([P, STEP_COLS], U32, tag="codes", align_bytes=64)
            scales = codes_pool.tile([P, STEP_COLS], U8, tag="scales", align_bytes=64)
            nc.vector.quantize_mx(out=codes[:].bitcast(FP8X4), scales=scales[:], in_=grouped)
            return codes, scales

        def multiply(weights, m):
            codes, scales = weights
            banks = []
            for first in range(0, HALF, 2):
                bank = product_pool.tile([P, 2, B], F32, tag="product")
                for s in range(2):
                    cols = slice((first + s) * P, (first + s + 1) * P)
                    nc.tensor.matmul_mx(
                        out=bank[:, s, :],
                        lhsT=codes[:, cols].bitcast(FP8X4),
                        lhsT_scale=scales[:, cols],
                        rhs=act_codes[:, m, :].bitcast(FP8X4),
                        rhs_scale=act_scales[:, m, :],
                        start=True,
                        stop=True,
                    )
                banks.append(bank)
            return banks

        def regroup(raw, s, engine, parts=1):
            grouped = grouped_pool.tile([P, HALF, P, PACK], BF16, tag="grouped", align_bytes=64)
            src = raw[:].rearrange("p f (v e) -> p f v e", e=E)[:, :, :, s * HALF : (s + 1) * HALF]
            for part in range(parts):
                units = slice(part * P // parts, (part + 1) * P // parts)
                copy(
                    grouped[:, :, units].rearrange("p e v f -> p v f e"),
                    src[:, :, units].rearrange("p f v e -> p v f e"),
                    engine,
                )
            return grouped

        own_grouped, own_weights, own_banks, own_gated = {}, {}, {}, {}

        def own_copy_in(k):
            own_grouped[k] = regroup(own_raw[k // 2], k % 2, OWN_ENGINES[k % len(OWN_ENGINES)], 2 if k < 2 else 1)

        def own_quantise(k):
            own_weights[k] = quantise(own_grouped[k][:].rearrange("p e v f -> p (e v f)"))

        def own_multiply(k):
            own_banks[k] = multiply(own_weights[k], k // STEPS)

        def own_gate(k):
            t, vt, s = k // STEPS, k % STEPS // 2, k % 2
            gated = gated_pool.tile([P, HALF, B], F32, tag="gated")
            for i in range(HALF):
                e = s * HALF + i
                nc.vector.scalar_tensor_tensor(
                    out=gated[:, i, :],
                    in0=own_banks[k][i // 2][:, i % 2, :],
                    scalar=minus_bias[:, t, vt, e : e + 1],
                    in1=spread_gates[:, t, e, :],
                    op0=ALU.max,
                    op1=ALU.mult,
                )
            own_gated[k] = gated

        sums = {}

        def add_bias_term(t, h, out_columns, first, start):
            nc.tensor.matmul(
                out=out_columns,
                lhsT=gate_rows[:, t * B_TILES + h, :],
                rhs=bias_moving[:, first : first + out_columns.shape[1]],
                start=start,
                stop=False,
            )

        def sum_columns(t, h, vt):
            if (t, vt) == (T - 1, V_TILES - 1):
                return last_bank[0][:, h, :]
            return sums[t, h][:, vt * P : (vt + 1) * P]

        last_bank = []

        def own_add(k):
            t, vt, s = k // STEPS, k % STEPS // 2, k % 2
            if k % STEPS == 0:
                for h in range(B_TILES):
                    bank = sums_pool.tile([P, V], F32, tag="sums", name="sum_bank")
                    width = V if t < T - 1 else V - P
                    add_bias_term(t, h, bank[:, 0:width], 0, True)
                    sums[t, h] = bank
            if k == ALL_STEPS - 2:
                bank = turned_pool.tile([P, B_TILES, P], F32, tag="turned", name="last_bank")
                for h in range(B_TILES):
                    add_bias_term(t, h, bank[:, h, :], V - P, h == 0)
                last_bank.append(bank)
            closes = k % STEPS == STEPS - 1 or k == ALL_STEPS - 3
            for i in range(HALF):
                for h in range(B_TILES):
                    nc.tensor.matmul(
                        out=sum_columns(t, h, vt),
                        lhsT=own_gated[k][:, i, h * P : (h + 1) * P],
                        rhs=identity[:],
                        is_transpose=True,
                        start=False,
                        stop=(closes and i == HALF - 1 and (k < ALL_STEPS - 1 or h == B_TILES - 1)),
                    )

        shared_grouped, shared_hidden = {}, {}
        hidden_by_sample = keep.tile([P, 2, Q, V], F32)

        def shared_copy_in(i):
            shared_grouped[i] = regroup(shared_raw[i // 2], i % 2, SHARED_ENGINES[i % len(SHARED_ENGINES)])

        def shared_multiply(i):
            vt, s = i // 2, i % 2
            weights = quantise(shared_grouped[i][:].rearrange("p e v f -> p (e v f)"))
            banks = multiply(weights, SHARED)
            hidden = work.tile([P, Q, HALF, QB], F32, tag="hidden")
            for e in range(HALF):
                nc.scalar.activation(
                    out=hidden[:, :, e, :],
                    in_=banks[e // 2][:, e % 2, :].rearrange("p (q b) -> p q b", b=QB),
                    func=ACT.Relu,
                    bias=shared_bias[:, vt, s * HALF + e : s * HALF + e + 1],
                    scale=1.0,
                )
            shared_hidden[i] = hidden

        def shared_turn(i):
            vt, s = i // 2, i % 2
            for first in range(0, Q, 4):
                bank = turned_pool.tile([P, 4, P], F32, tag="turned")
                for q in range(4):
                    nc.tensor.transpose(
                        out=bank[:, q, :],
                        in_=shared_hidden[i][:, first + q].rearrange("p e b -> p (e b)"),
                        identity=identity[:],
                    )
                dst = hidden_by_sample[:, s, first : first + 4, vt * P : (vt + 1) * P]
                nc.scalar.copy(out=dst, in_=bank[:])

        shared_sum = {}

        def shared_gate(q):
            bank = turned_pool.tile([P, V], F32, tag="turned")
            for s in range(2):
                nc.tensor.matmul(
                    out=bank[:],
                    lhsT=block_gates[:, s, q].rearrange("p t b -> p (t b)"),
                    rhs=hidden_by_sample[:, s, q, :],
                    start=(s == 0),
                    stop=(s == 1),
                )
            if q % 2 == 0:
                shared_sum[q // 2] = work.tile([P, 2, V], F32, tag="shared_sum", name="shared_sum")
            nc.scalar.copy(out=shared_sum[q // 2][:, q % 2, :], in_=bank[:])
            if q % 2 == 1:
                for t in range(T):
                    nc.scalar.dma_start(
                        out=out[t].rearrange("(q b) v -> b q v", b=QB)[:, q - 1 : q + 1, :],
                        in_=shared_sum[q // 2][t * QB : (t + 1) * QB],
                    )

        shared_part = {}

        def load_shared_part(t):
            part = work.tile([P, B_TILES, V], F32, tag="hidden", name="part")
            nc.sync.dma_start(out=part[:], in_=out[t].rearrange("(h p) v -> p h v", p=P))
            shared_part[t] = part

        own_part = {}

        def hold_own_part(t):
            own = work.tile([P, B_TILES, V], F32, tag="own", name="own")
            for h in range(B_TILES):
                nc.scalar.copy(out=own[:, h, :], in_=sums[t, h][:])
            own_part[t] = own

        def finish_last(vt_first, vt_last):
            t = T - 1
            cols = slice(vt_first * P, vt_last * P)
            result = work.tile([P, B_TILES, V], F32, tag="result", name="result")
            if vt_last == V_TILES:
                nc.vector.tensor_tensor(
                    out=result[:, :, cols], in0=last_bank[0][:], in1=shared_part[t][:, :, cols], op=ALU.add
                )
            else:
                for h in range(B_TILES):
                    nc.vector.tensor_tensor(
                        out=result[:, h, cols], in0=sums[t, h][:, cols], in1=shared_part[t][:, h, cols], op=ALU.add
                    )
            nc.sync.dma_start(
                out=out[t].rearrange("(h p) v -> p h v", p=P)[:, :, cols], in_=result[:, :, cols]
            )

        def finish(t):
            result = work.tile([P, B_TILES, V], F32, tag="result", name="result")
            if t in own_part:
                for h in range(B_TILES):
                    for half in range(2):
                        cols = slice(half * V // 2, (half + 1) * V // 2)
                        nc.gpsimd.tensor_tensor(
                            out=result[:, h, cols],
                            in0=own_part[t][:, h, cols],
                            in1=shared_part[t][:, h, cols],
                            op=ALU.add,
                        )
            else:
                for h in range(B_TILES):
                    nc.vector.tensor_tensor(
                        out=result[:, h, :], in0=sums[t, h][:], in1=shared_part[t][:, h, :], op=ALU.add
                    )
            nc.sync.dma_start(out=out[t].rearrange("(h p) v -> p h v", p=P), in_=result[:])

        LEAD = 3
        quantise_activations(0)
        make_own_gates()
        spread(0, 0, E)
        for slot in range(-LEAD, ALL_STEPS + 1):
            k = slot
            if 0 <= k + LEAD < ALL_STEPS:
                own_copy_in(k + LEAD)
            if 0 <= slot + 1 < 2 * V_TILES:
                shared_copy_in(slot + 1)
            if slot == -LEAD:
                park_gates()
                make_bias_term()
                quantise_activations(SHARED)
            if slot == -1:
                make_shared_gates()
            if 0 <= k + 2 < ALL_STEPS:
                own_quantise(k + 2)
            if 0 <= k + 1 < ALL_STEPS:
                own_multiply(k + 1)
            if 0 <= k < ALL_STEPS:
                own_gate(k)
            if 0 <= k - 1 < ALL_STEPS:
                own_add(k - 1)
            if 0 <= slot < 2 * V_TILES:
                shared_multiply(slot)
            if 0 <= slot - 1 < 2 * V_TILES:
                shared_turn(slot - 1)
            if slot % 2 == 0 and 0 <= slot < (T - 1) * 8:
                c = V_TILES + slot // 2
                if c < T * V_TILES:
                    own_raw[c] = load_chunk(ew1[c // V_TILES], c % V_TILES)
            if slot in (2, 4, 6):
                quantise_activations(slot // 2)
            if k - 1 in (STEPS - 1, 2 * STEPS - 1, 3 * STEPS - 1):
                hold_own_part((k - 1) // STEPS)
            if 10 <= slot < 10 + Q:
                shared_gate(slot - 10)
            if slot == 20:
                load_shared_part(0)
                load_shared_part(1)
            if slot == 22:
                finish(0)
                load_shared_part(2)
            if slot == 23:
                finish(1)
                load_shared_part(3)
            if k - 1 == 3 * STEPS + 1:
                finish(T - 2)
            if k - 1 == ALL_STEPS - 3:
                finish_last(0, V_TILES - 1)
            if k - 1 == ALL_STEPS - 1:
                finish_last(V_TILES - 1, V_TILES)
